import numpy as np
import ml_dtypes


def mxq(x, axis, fmt="e4m3"):
    dtype, down = {"e4m3": (ml_dtypes.float8_e4m3fn, 7), "e5m2": (ml_dtypes.float8_e5m2, 14)}[fmt]
    v = np.moveaxis(np.asarray(x, np.float32).astype(ml_dtypes.bfloat16).astype(np.float64), axis, -1)
    blocks = v.reshape(v.shape[:-1] + (-1, 32))
    amax = np.abs(blocks).max(-1, keepdims=True)
    byte = np.maximum(np.where(amax > 0, np.frexp(amax)[1] - 1 + 127, 0) - down, 1)
    scale = np.exp2(byte - 127.0)
    codes = (blocks / scale).astype(np.float32).astype(dtype).astype(np.float64)
    return np.moveaxis((codes * scale).reshape(v.shape), -1, axis)


WIDE = False


def mx_kscale(k):
    if not WIDE:
        return np.ones(k)
    levels = np.array([10, -10, 5, -5, 0])
    a = np.random.permutation(np.resize(levels, k // 512 * 4)).reshape(k // 512, 4)
    idx = np.arange(k)
    return np.exp2(a[idx // 512, idx % 128 // 32])


BF16 = ml_dtypes.bfloat16


def bf(x):
    return np.asarray(x, np.float32).astype(BF16)


def f64(x):
    return np.asarray(x).astype(np.float64)


B, S, H, HD, DX, NW = 1, 512, 8, 128, 1024, 4
D = H * HD


def split_heads(t):
    return t.reshape(B, S, H, HD).transpose(0, 2, 1, 3)


def merge_heads(t):
    return t.transpose(0, 2, 1, 3).reshape(B, S, D)


def setup_inputs():
    s = mx_kscale(DX)
    w = 1.0 / np.sqrt(DX)
    return {
        "x_real": bf(np.random.standard_normal((B, S, DX)) * s),
        "x_imag": bf(np.random.standard_normal((B, S, DX)) * s),
        "q_zeta_r": bf(np.random.standard_normal((B, H, S, HD)) * 1.2),
        "q_zeta_i": bf(np.random.standard_normal((B, H, S, HD)) * 1.2),
        "k_zeta_r": bf(np.random.standard_normal((B, H, S, HD)) * 1.2),
        "k_zeta_i": bf(np.random.standard_normal((B, H, S, HD)) * 1.2),
        "wv_r": bf(np.random.standard_normal((D, DX)) * w / s),
        "wv_i": bf(np.random.standard_normal((D, DX)) * w / s),
        "bv_r": bf(np.random.standard_normal(D) * 0.3),
        "bv_i": bf(np.random.standard_normal(D) * 0.3),
    }


def reference(x_real, x_imag, q_zeta_r, q_zeta_i, k_zeta_r, k_zeta_i, wv_r, wv_i, bv_r, bv_i):
    xr = mxq(f64(x_real), 2, "e4m3")
    xi = mxq(f64(x_imag), 2, "e4m3")
    wr = mxq(f64(wv_r), 1, "e4m3")
    wi = mxq(f64(wv_i), 1, "e4m3")
    v_r = (xr @ wr.T) - (xi @ wi.T) + f64(bv_r)
    v_i = (xr @ wi.T) + (xi @ wr.T) + f64(bv_i)
    qr, qi = f64(q_zeta_r), f64(q_zeta_i)
    krt = f64(k_zeta_r).transpose(0, 1, 3, 2)
    kit = f64(k_zeta_i).transpose(0, 1, 3, 2)
    s_r = (qr @ krt - qi @ kit) / np.sqrt(HD)
    s_i = (qr @ kit + qi @ krt) / np.sqrt(HD)
    m = np.sqrt(s_r ** 2 + s_i ** 2)
    e = np.exp(m - m.max(-1, keepdims=True))
    eq = mxq(e, 3, "e4m3")
    z = e.sum(-1, keepdims=True)
    o_r = (eq @ mxq(split_heads(v_r), 2, "e4m3")) / z
    o_i = (eq @ mxq(split_heads(v_i), 2, "e4m3")) / z
    return merge_heads(o_r), merge_heads(o_i)

@@ -1,0 +1,360 @@
+from contextlib import ExitStack
+
+import concourse.mybir as mybir
+from concourse.masks import make_identity
+
+F32 = mybir.dt.float32
+BF16 = mybir.dt.bfloat16
+U32 = mybir.dt.uint32
+U8 = mybir.dt.uint8
+FP8X4 = mybir.dt.float8_e4m3fn_x4
+FUNC = mybir.ActivationFunctionType
+ALU = mybir.AluOpType
+AXIS = mybir.AxisListType
+
+P = 128
+S = 512
+H = 8
+HD = 128
+DX = 1024
+D = H * HD
+PACK = 4
+TILES = S // P
+UNITS = H * TILES
+PASSES = DX // (P * PACK)
+HEADS_PER_LOAD = 2
+W_BUFS = H // HEADS_PER_LOAD
+X_FIRST_HEAD = 3
+
+XR, XI, XN = 0, 1, 2
+
+FLOPS = 4 * 2 * S * DX * D + 4 * H * 2 * S * S * HD + 2 * H * 2 * S * S * HD
+
+
+def transpose_words(nc, bank, rows, ident_f32):
+    words = rows.bitcast(F32)
+    for g in range(PASSES):
+        for u in range(2):
+            first = (2 * g + u) * P
+            nc.tensor.transpose(bank[:, g, u, :], words[:, first : first + P], ident_f32[:])
+
+
+def tile_covenantattention_pa_kernel(
+    tc, x_real, x_imag, q_zeta_r, q_zeta_i, k_zeta_r, k_zeta_i, wv_r, wv_i, bv_r, bv_i, out_0, out_1
+):
+    nc = tc.nc
+    with ExitStack() as ctx:
+        ctx.enter_context(tc.manual_schedule())
+        const = ctx.enter_context(tc.tile_pool(name="const", bufs=1))
+        keep = ctx.enter_context(tc.tile_pool(name="keep", bufs=1))
+
+        ident_bf = const.tile([P, P], BF16)
+        make_identity(nc, ident_bf[:])
+        ident_f32 = const.tile([P, P], F32)
+        make_identity(nc, ident_f32[:])
+        warm = const.tile([P, 1], F32)
+        nc.vector.memset(warm[:], 1.0)
+        nc.scalar.activation(out=warm[:], in_=warm[:], func=FUNC.Sqrt)
+
+        m_all = keep.tile([P, UNITS, S], F32)
+        max_all = keep.tile([P, UNITS], F32)
+        neg_max = keep.tile([P, UNITS], F32)
+        sum_all = keep.tile([P, UNITS], F32)
+        inv_sum = keep.tile([P, UNITS], F32)
+        x_codes = keep.tile([P, 3, TILES * PASSES * P], U32, align_bytes=64)
+        x_scales = keep.tile([P, 3, TILES * PASSES * P], U8, align_bytes=64)
+        w_codes = keep.tile([P, H, 2 * PASSES * P], U32, align_bytes=64)
+        w_scales = keep.tile([P, H, 2 * PASSES * P], U8, align_bytes=64)
+        bias_r = keep.tile([P, D], BF16)
+        bias_i = keep.tile([P, D], BF16)
+        bias = (bias_r, bias_i)
+        nc.gpsimd.dma_start(out=bias_r[:], in_=bv_r.partition_broadcast(P))
+        nc.gpsimd.dma_start(out=bias_i[:], in_=bv_i.partition_broadcast(P))
+
+        with ExitStack() as first:
+            raw = first.enter_context(tc.tile_pool(name="raw", bufs=1))
+            w_in = first.enter_context(tc.tile_pool(name="w_in", bufs=W_BUFS))
+            stage = first.enter_context(tc.tile_pool(name="stage", bufs=2))
+            squares = first.enter_context(tc.tile_pool(name="squares", bufs=3))
+            psum_s = first.enter_context(tc.psum_pool(name="psum_s", bufs=3))
+            psum_t = first.enter_context(tc.psum_pool(name="psum_t", bufs=2))
+
+            q_raw_r = raw.tile([P, H, S], BF16)
+            q_raw_i = raw.tile([P, H, S], BF16)
+            k_raw_r = raw.tile([P, UNITS, HD], BF16)
+            k_raw_i = raw.tile([P, UNITS, HD], BF16)
+            q_raw = (q_raw_r, q_raw_i)
+            k_raw = (k_raw_r, k_raw_i)
+            x_raw_r = raw.tile([P, TILES, DX], BF16)
+            x_raw_i = raw.tile([P, TILES, DX], BF16)
+            x_raw = (x_raw_r, x_raw_i)
+            w_raw = {}
+            q_t, k_t, k_i_neg = {}, {}, {}
+            s_r, s_i = {}, {}
+
+            def load_heads(h0):
+                h1 = h0 + HEADS_PER_LOAD
+                for c, src in enumerate((q_zeta_r, q_zeta_i)):
+                    view = src.rearrange("b h (p j) d -> p (b h) (j d)", j=TILES)
+                    nc.sync.dma_start(out=q_raw[c][:, h0:h1, :], in_=view[:, h0:h1, :])
+                for c, src in enumerate((k_zeta_r, k_zeta_i)):
+                    view = src.rearrange("b h (j p) d -> p (b h j) d", p=P)
+                    nc.sync.dma_start(
+                        out=k_raw[c][:, h0 * TILES : h1 * TILES, :],
+                        in_=view[:, h0 * TILES : h1 * TILES, :],
+                    )
+
+            def load_w(h):
+                w_raw[h] = w_in.tile([P, 2, DX], BF16, name="w_raw")
+                for c, src in enumerate((wv_r, wv_i)):
+                    nc.sync.dma_start(out=w_raw[h][:, c, :], in_=src[h * HD : (h + 1) * HD, :])
+
+            def transpose_qk(h):
+                q_bank = psum_t.tile([P, 2, S], BF16, tag="tp")
+                k_bank = psum_t.tile([P, 2, S], BF16, tag="tp")
+                for c in range(2):
+                    for j in range(TILES):
+                        cols = slice(j * P, (j + 1) * P)
+                        nc.tensor.transpose(q_bank[:, c, cols], q_raw[c][:, h, cols], ident_bf[:])
+                for c in range(2):
+                    for j in range(TILES):
+                        cols = slice(j * P, (j + 1) * P)
+                        nc.tensor.transpose(
+                            k_bank[:, c, cols], k_raw[c][:, h * TILES + j, :], ident_bf[:]
+                        )
+                q_t[h] = stage.tile([P, 2, S], BF16, name="q_t")
+                k_t[h] = stage.tile([P, 2, S], BF16, name="k_t")
+                k_i_neg[h] = stage.tile([P, S], BF16, name="k_i_neg")
+                nc.vector.tensor_copy(out=q_t[h][:], in_=q_bank[:])
+                nc.vector.tensor_copy(out=k_t[h][:], in_=k_bank[:])
+                nc.vector.tensor_scalar(
+                    out=k_i_neg[h][:], in0=k_t[h][:, 1, :], scalar1=-1.0, scalar2=None, op0=ALU.mult
+                )
+
+            def prepare_w(h):
+                w_grouped = stage.tile([P, 2, PASSES, P, PACK], BF16, align_bytes=64)
+                w_words = w_grouped[:].bitcast(F32)
+                banks = []
+                for c in range(2):
+                    w_bank = psum_t.tile([P, PASSES, 2, P], F32, tag="tp")
+                    transpose_words(nc, w_bank, w_raw[h][:, c, :], ident_f32)
+                    banks.append(w_bank)
+                nc.scalar.copy(out=w_words[:, 0, :, :, :], in_=banks[0][:].rearrange("p g u r -> p g r u"))
+                nc.vector.tensor_copy(out=w_words[:, 1, :, :, :], in_=banks[1][:].rearrange("p g u r -> p g r u"))
+                return w_grouped
+
+            def quantise_w(h, w_grouped):
+                nc.vector.quantize_mx(
+                    out=w_codes[:, h, :].bitcast(FP8X4),
+                    scales=w_scales[:, h, :],
+                    in_=w_grouped[:].rearrange("p c g r f -> p (c g r f)"),
+                )
+
+            def prepare_x(t):
+                cols = slice(t * PASSES * P, (t + 1) * PASSES * P)
+                grouped = []
+                banks = []
+                for c in range(2):
+                    x_bank = psum_t.tile([P, PASSES, 2, P], F32, tag="tp")
+                    transpose_words(nc, x_bank, x_raw[c][:, t, :], ident_f32)
+                    banks.append(x_bank)
+                    grouped.append(
+                        stage.tile([P, PASSES * P * PACK], BF16, name="x_grouped%d" % c, align_bytes=64)
+                    )
+                x_negated = stage.tile([P, PASSES * P * PACK], BF16, align_bytes=64)
+                for c, copy in enumerate((nc.scalar.copy, nc.vector.tensor_copy)):
+                    copy(
+                        out=grouped[c][:].bitcast(F32).rearrange("p (g r u) -> p g r u", g=PASSES, u=2),
+                        in_=banks[c][:].rearrange("p g u r -> p g r u"),
+                    )
+                nc.vector.quantize_mx(
+                    out=x_codes[:, XR, cols].bitcast(FP8X4), scales=x_scales[:, XR, cols], in_=grouped[XR][:]
+                )
+                nc.vector.tensor_scalar(
+                    out=x_negated[:], in0=grouped[XI][:], scalar1=-1.0, scalar2=None, op0=ALU.mult
+                )
+                nc.vector.quantize_mx(
+                    out=x_codes[:, XI, cols].bitcast(FP8X4), scales=x_scales[:, XI, cols], in_=grouped[XI][:]
+                )
+                nc.vector.quantize_mx(
+                    out=x_codes[:, XN, cols].bitcast(FP8X4), scales=x_scales[:, XN, cols], in_=x_negated[:]
+                )
+
+            def scores(unit):
+                h, j = divmod(unit, TILES)
+                cols = slice(j * P, (j + 1) * P)
+                s_r[unit] = psum_s.tile([P, S], F32, name="s_r")
+                s_i[unit] = psum_s.tile([P, S], F32, name="s_i")
+                q_r, q_i = q_t[h][:, 0, cols], q_t[h][:, 1, cols]
+                nc.tensor.matmul(s_r[unit][:], lhsT=q_r, rhs=k_t[h][:, 0, :], start=True, stop=False)
+                nc.tensor.matmul(s_i[unit][:], lhsT=q_r, rhs=k_t[h][:, 1, :], start=True, stop=False)
+                nc.tensor.matmul(s_r[unit][:], lhsT=q_i, rhs=k_i_neg[h][:], start=False, stop=True)
+                nc.tensor.matmul(s_i[unit][:], lhsT=q_i, rhs=k_t[h][:, 0, :], start=False, stop=True)
+
+            def squared_magnitude(unit):
+                sq_r = squares.tile([P, S], F32)
+                sq_i = squares.tile([P, S], F32)
+                nc.scalar.activation(out=sq_r[:], in_=s_r[unit][:], func=FUNC.Square)
+                nc.scalar.activation(out=sq_i[:], in_=s_i[unit][:], func=FUNC.Square)
+                nc.vector.tensor_tensor(out=m_all[:, unit, :], in0=sq_r[:], in1=sq_i[:], op=ALU.add)
+
+            def magnitude_and_maximum(unit):
+                m = m_all[:, unit, :]
+                nc.scalar.activation(out=m, in_=m, func=FUNC.Sqrt, scale=1.0 / HD)
+                nc.vector.tensor_reduce(out=max_all[:, unit : unit + 1], in_=m, axis=AXIS.X, op=ALU.max)
+                if unit % TILES == TILES - 1:
+                    head = slice(unit + 1 - TILES, unit + 1)
+                    nc.vector.tensor_scalar(
+                        out=neg_max[:, head], in0=max_all[:, head], scalar1=-1.0, scalar2=None, op0=ALU.mult
+                    )
+
+            for n in range(W_BUFS):
+                load_heads(n * HEADS_PER_LOAD)
+                load_w(n)
+            for c, src in enumerate((x_real, x_imag)):
+                nc.sync.dma_start(
+                    out=x_raw[c][:].rearrange("p (u e) k -> p u (e k)", e=2),
+                    in_=src.rearrange("b (u p e) k -> p (b u) (e k)", p=P, e=2),
+                )
+
+            transpose_qk(0)
+            for step in range(UNITS + 2):
+                h, j = divmod(step, TILES)
+                w_grouped = None
+                if step < UNITS:
+                    if j == 0:
+                        w_grouped = prepare_w(h)
+                        if h + W_BUFS < H:
+                            load_w(h + W_BUFS)
+                    if j == 1 and 0 <= h - X_FIRST_HEAD < TILES:
+                        prepare_x(h - X_FIRST_HEAD)
+                    if j == TILES - 1 and h + 1 < H:
+                        transpose_qk(h + 1)
+                    scores(step)
+                if 1 <= step <= UNITS:
+                    squared_magnitude(step - 1)
+                if step >= 2:
+                    magnitude_and_maximum(step - 2)
+                if w_grouped is not None:
+                    quantise_w(h, w_grouped)
+
+        with ExitStack() as second:
+            soft = second.enter_context(tc.tile_pool(name="soft", bufs=2, reuse_waits="tile"))
+            psum_e = second.enter_context(tc.psum_pool(name="psum_e", bufs=2, reuse_waits="tile"))
+            psum_v = second.enter_context(tc.psum_pool(name="psum_v", bufs=4, reuse_waits="tile"))
+            psum_o = second.enter_context(tc.psum_pool(name="psum_o", bufs=2, reuse_waits="tile"))
+            out_views = [o.rearrange("b (p j) f -> p (b j) f", j=TILES) for o in (out_0, out_1)]
+            e_sb, e_codes, e_scales, v_codes, v_scales = {}, {}, {}, {}, {}
+
+            def values(h):
+                v_grouped = soft.tile([P, 2, HD, PACK], BF16, align_bytes=64)
+                for c_out, products in enumerate((((XR, 0), (XN, 1)), ((XR, 1), (XI, 0)))):
+                    passes = [(x_sel, w_sel, g) for (x_sel, w_sel) in products for g in range(PASSES)]
+                    acc = psum_v.tile([P, TILES, HD], F32)
+                    for t in range(TILES):
+                        for i, (x_sel, w_sel, g) in enumerate(passes):
+                            x_cols = slice((t * PASSES + g) * P, (t * PASSES + g + 1) * P)
+                            w_cols = slice((w_sel * PASSES + g) * P, (w_sel * PASSES + g + 1) * P)
+                            nc.tensor.matmul_mx(
+                                out=acc[:, t, :],
+                                lhsT=x_codes[:, x_sel, x_cols].bitcast(FP8X4),
+                                lhsT_scale=x_scales[:, x_sel, x_cols],
+                                rhs=w_codes[:, h, w_cols].bitcast(FP8X4),
+                                rhs_scale=w_scales[:, h, w_cols],
+                                start=(i == 0),
+                                stop=(i == len(passes) - 1),
+                            )
+                    nc.vector.tensor_tensor(
+                        out=v_grouped[:, c_out, :, :],
+                        in0=acc[:].rearrange("p t f -> p f t"),
+                        in1=bias[c_out][:, h * HD : (h + 1) * HD].unsqueeze(2).to_broadcast([P, HD, PACK]),
+                        op=ALU.add,
+                    )
+                v_codes[h] = soft.tile([P, 2 * HD], U32, name="v_codes", align_bytes=64)
+                v_scales[h] = soft.tile([P, 2 * HD], U8, name="v_scales", align_bytes=64)
+                nc.vector.quantize_mx(
+                    out=v_codes[h][:].bitcast(FP8X4),
+                    scales=v_scales[h][:],
+                    in_=v_grouped[:].rearrange("p c f t -> p (c f t)"),
+                )
+
+            def exponentials(h):
+                e_sb[h] = soft.tile([P, TILES, S], BF16, name="e_sb")
+                for j in range(TILES):
+                    unit = h * TILES + j
+                    nc.scalar.activation(
+                        out=e_sb[h][:, j, :],
+                        in_=m_all[:, unit, :],
+                        func=FUNC.Exp,
+                        bias=neg_max[:, unit : unit + 1],
+                        accum_out=sum_all[:, unit : unit + 1],
+                    )
+
+            def transpose_e(h):
+                e_words = e_sb[h][:].bitcast(F32)
+                e_grouped = soft.tile([P, TILES, P, PACK], BF16, align_bytes=64)
+                e_grouped_words = e_grouped[:].bitcast(F32)
+                for j0 in range(0, TILES, 2):
+                    e_bank = psum_e.tile([P, 2, 2, P], F32)
+                    for jj in range(2):
+                        for u in range(2):
+                            nc.tensor.transpose(
+                                e_bank[:, jj, u, :], e_words[:, j0 + jj, u * P : (u + 1) * P], ident_f32[:]
+                            )
+                    nc.vector.tensor_copy(
+                        out=e_grouped_words[:, j0 : j0 + 2, :, :],
+                        in_=e_bank[:].rearrange("p j u q -> p j q u"),
+                    )
+                units = slice(h * TILES, (h + 1) * TILES)
+                nc.vector.reciprocal(out=inv_sum[:, units], in_=sum_all[:, units])
+                e_codes[h] = soft.tile([P, S], U32, name="e_codes", align_bytes=64)
+                e_scales[h] = soft.tile([P, S], U8, name="e_scales", align_bytes=64)
+                nc.vector.quantize_mx(
+                    out=e_codes[h][:].bitcast(FP8X4),
+                    scales=e_scales[h][:],
+                    in_=e_grouped[:].rearrange("p j q f -> p (j q f)"),
+                )
+
+            def weighted_sums(h):
+                o_sb = soft.tile([P, TILES, 2, HD], F32)
+                o_banks = []
+                for j0 in range(0, TILES, 2):
+                    o_bank = psum_o.tile([P, 2, 2 * HD], F32)
+                    for jj in range(2):
+                        cols = slice((j0 + jj) * P, (j0 + jj + 1) * P)
+                        nc.tensor.matmul_mx(
+                            out=o_bank[:, jj, :],
+                            lhsT=e_codes[h][:, cols].bitcast(FP8X4),
+                            lhsT_scale=e_scales[h][:, cols],
+                            rhs=v_codes[h][:].bitcast(FP8X4),
+                            rhs_scale=v_scales[h][:],
+                            start=True,
+                            stop=True,
+                        )
+                    o_banks.append(o_bank)
+                for jj in range(2):
+                    unit = h * TILES + jj
+                    nc.scalar.activation(
+                        out=o_sb[:, jj, :, :].rearrange("p c d -> p (c d)"),
+                        in_=o_banks[0][:, jj, :],
+                        func=FUNC.Copy,
+                        scale=inv_sum[:, unit : unit + 1],
+                    )
+                unit = h * TILES + 2
+                nc.vector.tensor_tensor(
+                    out=o_sb[:, 2:TILES, :, :].rearrange("p j c d -> p j (c d)"),
+                    in0=o_banks[1][:],
+                    in1=inv_sum[:, unit : unit + 2].unsqueeze(2).to_broadcast([P, 2, 2 * HD]),
+                    op=ALU.mult,
+                )
+                for c in range(2):
+                    nc.sync.dma_start(out=out_views[c][:, :, h * HD : (h + 1) * HD], in_=o_sb[:, :, c, :])
+
+            exponentials(0)
+            values(0)
+            for h in range(H):
+                transpose_e(h)
+                if h + 1 < H:
+                    exponentials(h + 1)
+                    values(h + 1)
+                weighted_sums(h)

@@ -22,8 +22,7 @@ PACK = 4
 TILES = S // P
 UNITS = H * TILES
 PASSES = DX // (P * PACK)
-HEADS_PER_LOAD = 2
-W_BUFS = H // HEADS_PER_LOAD
+W_BUFS = 4
 X_FIRST_HEAD = 3
 
 XR, XI, XN = 0, 1, 2
@@ -68,16 +67,14 @@ def tile_covenantattention_pa_kernel(
         bias_r = keep.tile([P, D], BF16)
         bias_i = keep.tile([P, D], BF16)
         bias = (bias_r, bias_i)
-        nc.gpsimd.dma_start(out=bias_r[:], in_=bv_r.partition_broadcast(P))
-        nc.gpsimd.dma_start(out=bias_i[:], in_=bv_i.partition_broadcast(P))
 
         with ExitStack() as first:
             raw = first.enter_context(tc.tile_pool(name="raw", bufs=1))
             w_in = first.enter_context(tc.tile_pool(name="w_in", bufs=W_BUFS))
             stage = first.enter_context(tc.tile_pool(name="stage", bufs=2))
-            squares = first.enter_context(tc.tile_pool(name="squares", bufs=3))
-            psum_s = first.enter_context(tc.psum_pool(name="psum_s", bufs=3))
-            psum_t = first.enter_context(tc.psum_pool(name="psum_t", bufs=2))
+            squares = first.enter_context(tc.tile_pool(name="squares", bufs=4))
+            psum_s = first.enter_context(tc.psum_pool(name="psum_s", bufs=2))
+            psum_t = first.enter_context(tc.psum_pool(name="psum_t", bufs=4))
 
             q_raw_r = raw.tile([P, H, S], BF16)
             q_raw_i = raw.tile([P, H, S], BF16)
@@ -92,17 +89,14 @@ def tile_covenantattention_pa_kernel(
             q_t, k_t, k_i_neg = {}, {}, {}
             s_r, s_i = {}, {}
 
-            def load_heads(h0):
-                h1 = h0 + HEADS_PER_LOAD
-                for c, src in enumerate((q_zeta_r, q_zeta_i)):
-                    view = src.rearrange("b h (p j) d -> p (b h) (j d)", j=TILES)
-                    nc.sync.dma_start(out=q_raw[c][:, h0:h1, :], in_=view[:, h0:h1, :])
+            def load_qk(h):
                 for c, src in enumerate((k_zeta_r, k_zeta_i)):
                     view = src.rearrange("b h (j p) d -> p (b h j) d", p=P)
-                    nc.sync.dma_start(
-                        out=k_raw[c][:, h0 * TILES : h1 * TILES, :],
-                        in_=view[:, h0 * TILES : h1 * TILES, :],
-                    )
+                    units = slice(h * TILES, (h + 1) * TILES)
+                    nc.sync.dma_start(out=k_raw[c][:, units, :], in_=view[:, units, :])
+                for c, src in enumerate((q_zeta_r, q_zeta_i)):
+                    view = src.rearrange("b h (p j) d -> p (b h) (j d)", j=TILES)
+                    nc.sync.dma_start(out=q_raw[c][:, h, :], in_=view[:, h, :])
 
             def load_w(h):
                 w_raw[h] = w_in.tile([P, 2, DX], BF16, name="w_raw")
@@ -115,21 +109,21 @@ def tile_covenantattention_pa_kernel(
                 for c in range(2):
                     for j in range(TILES):
                         cols = slice(j * P, (j + 1) * P)
-                        nc.tensor.transpose(q_bank[:, c, cols], q_raw[c][:, h, cols], ident_bf[:])
-                for c in range(2):
-                    for j in range(TILES):
-                        cols = slice(j * P, (j + 1) * P)
                         nc.tensor.transpose(
                             k_bank[:, c, cols], k_raw[c][:, h * TILES + j, :], ident_bf[:]
                         )
+                for c in range(2):
+                    for j in range(TILES):
+                        cols = slice(j * P, (j + 1) * P)
+                        nc.tensor.transpose(q_bank[:, c, cols], q_raw[c][:, h, cols], ident_bf[:])
                 q_t[h] = stage.tile([P, 2, S], BF16, name="q_t")
                 k_t[h] = stage.tile([P, 2, S], BF16, name="k_t")
                 k_i_neg[h] = stage.tile([P, S], BF16, name="k_i_neg")
-                nc.vector.tensor_copy(out=q_t[h][:], in_=q_bank[:])
                 nc.vector.tensor_copy(out=k_t[h][:], in_=k_bank[:])
                 nc.vector.tensor_scalar(
                     out=k_i_neg[h][:], in0=k_t[h][:, 1, :], scalar1=-1.0, scalar2=None, op0=ALU.mult
                 )
+                nc.vector.tensor_copy(out=q_t[h][:], in_=q_bank[:])
 
             def prepare_w(h):
                 w_grouped = stage.tile([P, 2, PASSES, P, PACK], BF16, align_bytes=64)
@@ -139,7 +133,7 @@ def tile_covenantattention_pa_kernel(
                     w_bank = psum_t.tile([P, PASSES, 2, P], F32, tag="tp")
                     transpose_words(nc, w_bank, w_raw[h][:, c, :], ident_f32)
                     banks.append(w_bank)
-                nc.scalar.copy(out=w_words[:, 0, :, :, :], in_=banks[0][:].rearrange("p g u r -> p g r u"))
+                nc.vector.tensor_copy(out=w_words[:, 0, :, :, :], in_=banks[0][:].rearrange("p g u r -> p g r u"))
                 nc.vector.tensor_copy(out=w_words[:, 1, :, :, :], in_=banks[1][:].rearrange("p g u r -> p g r u"))
                 return w_grouped
 
@@ -162,7 +156,7 @@ def tile_covenantattention_pa_kernel(
                         stage.tile([P, PASSES * P * PACK], BF16, name="x_grouped%d" % c, align_bytes=64)
                     )
                 x_negated = stage.tile([P, PASSES * P * PACK], BF16, align_bytes=64)
-                for c, copy in enumerate((nc.scalar.copy, nc.vector.tensor_copy)):
+                for c, copy in enumerate((nc.vector.tensor_copy, nc.vector.tensor_copy)):
                     copy(
                         out=grouped[c][:].bitcast(F32).rearrange("p (g r u) -> p g r u", g=PASSES, u=2),
                         in_=banks[c][:].rearrange("p g u r -> p g r u"),
@@ -196,11 +190,14 @@ def tile_covenantattention_pa_kernel(
                 sq_i = squares.tile([P, S], F32)
                 nc.scalar.activation(out=sq_r[:], in_=s_r[unit][:], func=FUNC.Square)
                 nc.scalar.activation(out=sq_i[:], in_=s_i[unit][:], func=FUNC.Square)
-                nc.vector.tensor_tensor(out=m_all[:, unit, :], in0=sq_r[:], in1=sq_i[:], op=ALU.add)
+                nc.gpsimd.tensor_tensor(out=m_all[:, unit, :], in0=sq_r[:], in1=sq_i[:], op=ALU.add)
 
-            def magnitude_and_maximum(unit):
+            def magnitude(unit):
                 m = m_all[:, unit, :]
                 nc.scalar.activation(out=m, in_=m, func=FUNC.Sqrt, scale=1.0 / HD)
+
+            def maximum(unit):
+                m = m_all[:, unit, :]
                 nc.vector.tensor_reduce(out=max_all[:, unit : unit + 1], in_=m, axis=AXIS.X, op=ALU.max)
                 if unit % TILES == TILES - 1:
                     head = slice(unit + 1 - TILES, unit + 1)
@@ -208,43 +205,49 @@ def tile_covenantattention_pa_kernel(
                         out=neg_max[:, head], in0=max_all[:, head], scalar1=-1.0, scalar2=None, op0=ALU.mult
                     )
 
-            for n in range(W_BUFS):
-                load_heads(n * HEADS_PER_LOAD)
-                load_w(n)
+            for h in range(W_BUFS):
+                load_qk(h)
+                load_w(h)
             for c, src in enumerate((x_real, x_imag)):
                 nc.sync.dma_start(
                     out=x_raw[c][:].rearrange("p (u e) k -> p u (e k)", e=2),
                     in_=src.rearrange("b (u p e) k -> p (b u) (e k)", p=P, e=2),
                 )
+            for h in range(W_BUFS, H):
+                load_qk(h)
+            nc.sync.dma_start(out=bias_r[:], in_=bv_r.partition_broadcast(P))
+            nc.sync.dma_start(out=bias_i[:], in_=bv_i.partition_broadcast(P))
 
             transpose_qk(0)
-            for step in range(UNITS + 2):
+            for step in range(UNITS + 4):
                 h, j = divmod(step, TILES)
                 w_grouped = None
                 if step < UNITS:
-                    if j == 0:
+                    if j == 3:
                         w_grouped = prepare_w(h)
                         if h + W_BUFS < H:
                             load_w(h + W_BUFS)
-                    if j == 1 and 0 <= h - X_FIRST_HEAD < TILES:
+                    if j == 0 and 0 <= h - X_FIRST_HEAD < TILES:
                         prepare_x(h - X_FIRST_HEAD)
-                    if j == TILES - 1 and h + 1 < H:
+                    if j == 1 and h + 1 < H:
                         transpose_qk(h + 1)
                     scores(step)
                 if 1 <= step <= UNITS:
                     squared_magnitude(step - 1)
-                if step >= 2:
-                    magnitude_and_maximum(step - 2)
+                if 3 <= step < UNITS + 3:
+                    magnitude(step - 3)
+                if step >= 4:
+                    maximum(step - 4)
                 if w_grouped is not None:
                     quantise_w(h, w_grouped)
 
         with ExitStack() as second:
             soft = second.enter_context(tc.tile_pool(name="soft", bufs=2, reuse_waits="tile"))
             psum_e = second.enter_context(tc.psum_pool(name="psum_e", bufs=2, reuse_waits="tile"))
-            psum_v = second.enter_context(tc.psum_pool(name="psum_v", bufs=4, reuse_waits="tile"))
-            psum_o = second.enter_context(tc.psum_pool(name="psum_o", bufs=2, reuse_waits="tile"))
+            psum_v = second.enter_context(tc.psum_pool(name="psum_v", bufs=2, reuse_waits="tile"))
+            psum_o = second.enter_context(tc.psum_pool(name="psum_o", bufs=4, reuse_waits="tile"))
             out_views = [o.rearrange("b (p j) f -> p (b j) f", j=TILES) for o in (out_0, out_1)]
-            e_sb, e_codes, e_scales, v_codes, v_scales = {}, {}, {}, {}, {}
+            e_sb, e_codes, e_scales, v_codes, v_scales, o_banks = {}, {}, {}, {}, {}, {}
 
             def values(h):
                 v_grouped = soft.tile([P, 2, HD, PACK], BF16, align_bytes=64)
@@ -316,8 +319,7 @@ def tile_covenantattention_pa_kernel(
                 )
 
             def weighted_sums(h):
-                o_sb = soft.tile([P, TILES, 2, HD], F32)
-                o_banks = []
+                o_banks[h] = []
                 for j0 in range(0, TILES, 2):
                     o_bank = psum_o.tile([P, 2, 2 * HD], F32)
                     for jj in range(2):
@@ -331,19 +333,22 @@ def tile_covenantattention_pa_kernel(
                             start=True,
                             stop=True,
                         )
-                    o_banks.append(o_bank)
+                    o_banks[h].append(o_bank)
+
+            def normalise_and_store(h):
+                o_sb = soft.tile([P, TILES, 2, HD], F32, bufs=4)
                 for jj in range(2):
                     unit = h * TILES + jj
                     nc.scalar.activation(
                         out=o_sb[:, jj, :, :].rearrange("p c d -> p (c d)"),
-                        in_=o_banks[0][:, jj, :],
+                        in_=o_banks[h][0][:, jj, :],
                         func=FUNC.Copy,
                         scale=inv_sum[:, unit : unit + 1],
                     )
                 unit = h * TILES + 2
                 nc.vector.tensor_tensor(
                     out=o_sb[:, 2:TILES, :, :].rearrange("p j c d -> p j (c d)"),
-                    in0=o_banks[1][:],
+                    in0=o_banks[h][1][:],
                     in1=inv_sum[:, unit : unit + 2].unsqueeze(2).to_broadcast([P, 2, 2 * HD]),
                     op=ALU.mult,
                 )
@@ -358,3 +363,6 @@ def tile_covenantattention_pa_kernel(
                     exponentials(h + 1)
                     values(h + 1)
                 weighted_sums(h)
+                if h >= 1:
+                    normalise_and_store(h - 1)
+            normalise_and_store(H - 1)

@@ -22,10 +22,16 @@ PACK = 4
 TILES = S // P
 UNITS = H * TILES
 PASSES = DX // (P * PACK)
-W_BUFS = 4
-X_FIRST_HEAD = 3
+PASS_COLS = PASSES * P
 
 XR, XI, XN = 0, 1, 2
+
+W_BUFS = 4
+SQUARE_LAG = 1
+SQRT_LAG = 3
+MAX_LAG = 4
+X_SLOT, QK_SLOT, W_SLOT = 0, 1, 3
+X_FIRST_HEAD = 3
 
 FLOPS = 4 * 2 * S * DX * D + 4 * H * 2 * S * S * HD + 2 * H * 2 * S * S * HD
 
@@ -36,6 +42,13 @@ def transpose_words(nc, bank, rows, ident_f32):
         for u in range(2):
             first = (2 * g + u) * P
             nc.tensor.transpose(bank[:, g, u, :], words[:, first : first + P], ident_f32[:])
+
+
+def regroup_words(nc, grouped, bank):
+    nc.vector.tensor_copy(
+        out=grouped.bitcast(F32).rearrange("p (g r u) -> p g r u", g=PASSES, u=2),
+        in_=bank[:].rearrange("p g u r -> p g r u"),
+    )
 
 
 def tile_covenantattention_pa_kernel(
@@ -60,10 +73,10 @@ def tile_covenantattention_pa_kernel(
         neg_max = keep.tile([P, UNITS], F32)
         sum_all = keep.tile([P, UNITS], F32)
         inv_sum = keep.tile([P, UNITS], F32)
-        x_codes = keep.tile([P, 3, TILES * PASSES * P], U32, align_bytes=64)
-        x_scales = keep.tile([P, 3, TILES * PASSES * P], U8, align_bytes=64)
-        w_codes = keep.tile([P, H, 2 * PASSES * P], U32, align_bytes=64)
-        w_scales = keep.tile([P, H, 2 * PASSES * P], U8, align_bytes=64)
+        x_codes = keep.tile([P, 3, TILES * PASS_COLS], U32, align_bytes=64)
+        x_scales = keep.tile([P, 3, TILES * PASS_COLS], U8, align_bytes=64)
+        w_codes = keep.tile([P, H, 2 * PASS_COLS], U32, align_bytes=64)
+        w_scales = keep.tile([P, H, 2 * PASS_COLS], U8, align_bytes=64)
         bias_r = keep.tile([P, D], BF16)
         bias_i = keep.tile([P, D], BF16)
         bias = (bias_r, bias_i)
@@ -80,14 +93,15 @@ def tile_covenantattention_pa_kernel(
             q_raw_i = raw.tile([P, H, S], BF16)
             k_raw_r = raw.tile([P, UNITS, HD], BF16)
             k_raw_i = raw.tile([P, UNITS, HD], BF16)
-            q_raw = (q_raw_r, q_raw_i)
-            k_raw = (k_raw_r, k_raw_i)
             x_raw_r = raw.tile([P, TILES, DX], BF16)
             x_raw_i = raw.tile([P, TILES, DX], BF16)
+            x_grouped_r = raw.tile([P, TILES, PASS_COLS * PACK], BF16, align_bytes=64)
+            x_grouped_i = raw.tile([P, TILES, PASS_COLS * PACK], BF16, align_bytes=64)
+            q_raw = (q_raw_r, q_raw_i)
+            k_raw = (k_raw_r, k_raw_i)
             x_raw = (x_raw_r, x_raw_i)
-            w_raw = {}
-            q_t, k_t, k_i_neg = {}, {}, {}
-            s_r, s_i = {}, {}
+            x_grouped = (x_grouped_r, x_grouped_i)
+            w_raw, w_grouped, q_t, k_t, k_i_neg, s_r, s_i = {}, {}, {}, {}, {}, {}, {}
 
             def load_qk(h):
                 for c, src in enumerate((k_zeta_r, k_zeta_i)):
@@ -104,82 +118,69 @@ def tile_covenantattention_pa_kernel(
                     nc.sync.dma_start(out=w_raw[h][:, c, :], in_=src[h * HD : (h + 1) * HD, :])
 
             def transpose_qk(h):
-                q_bank = psum_t.tile([P, 2, S], BF16, tag="tp")
-                k_bank = psum_t.tile([P, 2, S], BF16, tag="tp")
+                k_bank = psum_t.tile([P, 2, S], BF16, tag="bank")
+                q_bank = psum_t.tile([P, 2, S], BF16, tag="bank")
                 for c in range(2):
                     for j in range(TILES):
-                        cols = slice(j * P, (j + 1) * P)
                         nc.tensor.transpose(
-                            k_bank[:, c, cols], k_raw[c][:, h * TILES + j, :], ident_bf[:]
+                            k_bank[:, c, j * P : (j + 1) * P], k_raw[c][:, h * TILES + j, :], ident_bf[:]
                         )
                 for c in range(2):
                     for j in range(TILES):
                         cols = slice(j * P, (j + 1) * P)
                         nc.tensor.transpose(q_bank[:, c, cols], q_raw[c][:, h, cols], ident_bf[:])
-                q_t[h] = stage.tile([P, 2, S], BF16, name="q_t")
                 k_t[h] = stage.tile([P, 2, S], BF16, name="k_t")
                 k_i_neg[h] = stage.tile([P, S], BF16, name="k_i_neg")
+                q_t[h] = stage.tile([P, 2, S], BF16, name="q_t")
                 nc.vector.tensor_copy(out=k_t[h][:], in_=k_bank[:])
                 nc.vector.tensor_scalar(
-                    out=k_i_neg[h][:], in0=k_t[h][:, 1, :], scalar1=-1.0, scalar2=None, op0=ALU.mult
+                    out=k_i_neg[h][:], in0=k_bank[:, 1, :], scalar1=-1.0, scalar2=None, op0=ALU.mult
                 )
                 nc.vector.tensor_copy(out=q_t[h][:], in_=q_bank[:])
 
             def prepare_w(h):
-                w_grouped = stage.tile([P, 2, PASSES, P, PACK], BF16, align_bytes=64)
-                w_words = w_grouped[:].bitcast(F32)
+                w_grouped[h] = stage.tile([P, 2, PASS_COLS * PACK], BF16, name="w_grouped", align_bytes=64)
                 banks = []
                 for c in range(2):
-                    w_bank = psum_t.tile([P, PASSES, 2, P], F32, tag="tp")
+                    w_bank = psum_t.tile([P, PASSES, 2, P], F32, tag="bank")
                     transpose_words(nc, w_bank, w_raw[h][:, c, :], ident_f32)
                     banks.append(w_bank)
-                nc.vector.tensor_copy(out=w_words[:, 0, :, :, :], in_=banks[0][:].rearrange("p g u r -> p g r u"))
-                nc.vector.tensor_copy(out=w_words[:, 1, :, :, :], in_=banks[1][:].rearrange("p g u r -> p g r u"))
-                return w_grouped
+                for c in range(2):
+                    regroup_words(nc, w_grouped[h][:, c, :], banks[c])
 
-            def quantise_w(h, w_grouped):
+            def quantise_w(h):
                 nc.vector.quantize_mx(
                     out=w_codes[:, h, :].bitcast(FP8X4),
                     scales=w_scales[:, h, :],
-                    in_=w_grouped[:].rearrange("p c g r f -> p (c g r f)"),
+                    in_=w_grouped[h][:].rearrange("p c w -> p (c w)"),
                 )
 
             def prepare_x(t):
-                cols = slice(t * PASSES * P, (t + 1) * PASSES * P)
-                grouped = []
                 banks = []
                 for c in range(2):
-                    x_bank = psum_t.tile([P, PASSES, 2, P], F32, tag="tp")
+                    x_bank = psum_t.tile([P, PASSES, 2, P], F32, tag="bank")
                     transpose_words(nc, x_bank, x_raw[c][:, t, :], ident_f32)
                     banks.append(x_bank)
-                    grouped.append(
-                        stage.tile([P, PASSES * P * PACK], BF16, name="x_grouped%d" % c, align_bytes=64)
-                    )
-                x_negated = stage.tile([P, PASSES * P * PACK], BF16, align_bytes=64)
-                for c, copy in enumerate((nc.vector.tensor_copy, nc.vector.tensor_copy)):
-                    copy(
-                        out=grouped[c][:].bitcast(F32).rearrange("p (g r u) -> p g r u", g=PASSES, u=2),
-                        in_=banks[c][:].rearrange("p g u r -> p g r u"),
-                    )
+                for c in range(2):
+                    regroup_words(nc, x_grouped[c][:, t, :], banks[c])
+
+            def quantise_x(x_sel):
+                flat_r = x_grouped_r[:].rearrange("p t w -> p (t w)")
+                flat_i = x_grouped_i[:].rearrange("p t w -> p (t w)")
+                if x_sel == XN:
+                    nc.vector.tensor_scalar(out=flat_r, in0=flat_i, scalar1=-1.0, scalar2=None, op0=ALU.mult)
                 nc.vector.quantize_mx(
-                    out=x_codes[:, XR, cols].bitcast(FP8X4), scales=x_scales[:, XR, cols], in_=grouped[XR][:]
-                )
-                nc.vector.tensor_scalar(
-                    out=x_negated[:], in0=grouped[XI][:], scalar1=-1.0, scalar2=None, op0=ALU.mult
-                )
-                nc.vector.quantize_mx(
-                    out=x_codes[:, XI, cols].bitcast(FP8X4), scales=x_scales[:, XI, cols], in_=grouped[XI][:]
-                )
-                nc.vector.quantize_mx(
-                    out=x_codes[:, XN, cols].bitcast(FP8X4), scales=x_scales[:, XN, cols], in_=x_negated[:]
+                    out=x_codes[:, x_sel, :].bitcast(FP8X4),
+                    scales=x_scales[:, x_sel, :],
+                    in_=flat_i if x_sel == XI else flat_r,
                 )
 
             def scores(unit):
                 h, j = divmod(unit, TILES)
-                cols = slice(j * P, (j + 1) * P)
+                q_r = q_t[h][:, 0, j * P : (j + 1) * P]
+                q_i = q_t[h][:, 1, j * P : (j + 1) * P]
                 s_r[unit] = psum_s.tile([P, S], F32, name="s_r")
                 s_i[unit] = psum_s.tile([P, S], F32, name="s_i")
-                q_r, q_i = q_t[h][:, 0, cols], q_t[h][:, 1, cols]
                 nc.tensor.matmul(s_r[unit][:], lhsT=q_r, rhs=k_t[h][:, 0, :], start=True, stop=False)
                 nc.tensor.matmul(s_i[unit][:], lhsT=q_r, rhs=k_t[h][:, 1, :], start=True, stop=False)
                 nc.tensor.matmul(s_r[unit][:], lhsT=q_i, rhs=k_i_neg[h][:], start=False, stop=True)
@@ -197,8 +198,9 @@ def tile_covenantattention_pa_kernel(
                 nc.scalar.activation(out=m, in_=m, func=FUNC.Sqrt, scale=1.0 / HD)
 
             def maximum(unit):
-                m = m_all[:, unit, :]
-                nc.vector.tensor_reduce(out=max_all[:, unit : unit + 1], in_=m, axis=AXIS.X, op=ALU.max)
+                nc.vector.tensor_reduce(
+                    out=max_all[:, unit : unit + 1], in_=m_all[:, unit, :], axis=AXIS.X, op=ALU.max
+                )
                 if unit % TILES == TILES - 1:
                     head = slice(unit + 1 - TILES, unit + 1)
                     nc.vector.tensor_scalar(
@@ -218,28 +220,30 @@ def tile_covenantattention_pa_kernel(
             nc.sync.dma_start(out=bias_r[:], in_=bv_r.partition_broadcast(P))
             nc.sync.dma_start(out=bias_i[:], in_=bv_i.partition_broadcast(P))
 
+            x_done = (X_FIRST_HEAD + TILES - 1) * TILES + X_SLOT
             transpose_qk(0)
-            for step in range(UNITS + 4):
+            for step in range(UNITS + MAX_LAG):
                 h, j = divmod(step, TILES)
-                w_grouped = None
                 if step < UNITS:
-                    if j == 3:
-                        w_grouped = prepare_w(h)
+                    if j == X_SLOT and 0 <= h - X_FIRST_HEAD < TILES:
+                        prepare_x(h - X_FIRST_HEAD)
+                    if j == QK_SLOT and h + 1 < H:
+                        transpose_qk(h + 1)
+                    if j == W_SLOT:
+                        prepare_w(h)
                         if h + W_BUFS < H:
                             load_w(h + W_BUFS)
-                    if j == 0 and 0 <= h - X_FIRST_HEAD < TILES:
-                        prepare_x(h - X_FIRST_HEAD)
-                    if j == 1 and h + 1 < H:
-                        transpose_qk(h + 1)
                     scores(step)
-                if 1 <= step <= UNITS:
-                    squared_magnitude(step - 1)
-                if 3 <= step < UNITS + 3:
-                    magnitude(step - 3)
-                if step >= 4:
-                    maximum(step - 4)
-                if w_grouped is not None:
-                    quantise_w(h, w_grouped)
+                if 0 <= step - SQUARE_LAG < UNITS:
+                    squared_magnitude(step - SQUARE_LAG)
+                if 0 <= step - SQRT_LAG < UNITS:
+                    magnitude(step - SQRT_LAG)
+                if 0 <= step - MAX_LAG < UNITS:
+                    maximum(step - MAX_LAG)
+                if step < UNITS and j == W_SLOT:
+                    quantise_w(h)
+                if 0 <= step - x_done < 3:
+                    quantise_x(step - x_done)
 
         with ExitStack() as second:
             soft = second.enter_context(tc.tile_pool(name="soft", bufs=2, reuse_waits="tile"))
@@ -294,9 +298,11 @@ def tile_covenantattention_pa_kernel(
                     )
 
             def transpose_e(h):
+                units = slice(h * TILES, (h + 1) * TILES)
+                nc.vector.reciprocal(out=inv_sum[:, units], in_=sum_all[:, units])
                 e_words = e_sb[h][:].bitcast(F32)
-                e_grouped = soft.tile([P, TILES, P, PACK], BF16, align_bytes=64)
-                e_grouped_words = e_grouped[:].bitcast(F32)
+                e_codes[h] = soft.tile([P, S], U32, name="e_codes", align_bytes=64)
+                e_scales[h] = soft.tile([P, S], U8, name="e_scales", align_bytes=64)
                 for j0 in range(0, TILES, 2):
                     e_bank = psum_e.tile([P, 2, 2, P], F32)
                     for jj in range(2):
@@ -304,19 +310,16 @@ def tile_covenantattention_pa_kernel(
                             nc.tensor.transpose(
                                 e_bank[:, jj, u, :], e_words[:, j0 + jj, u * P : (u + 1) * P], ident_f32[:]
                             )
+                    e_grouped = soft.tile([P, 2, P, PACK], BF16, align_bytes=64)
                     nc.vector.tensor_copy(
-                        out=e_grouped_words[:, j0 : j0 + 2, :, :],
-                        in_=e_bank[:].rearrange("p j u q -> p j q u"),
+                        out=e_grouped[:].bitcast(F32), in_=e_bank[:].rearrange("p j u q -> p j q u")
                     )
-                units = slice(h * TILES, (h + 1) * TILES)
-                nc.vector.reciprocal(out=inv_sum[:, units], in_=sum_all[:, units])
-                e_codes[h] = soft.tile([P, S], U32, name="e_codes", align_bytes=64)
-                e_scales[h] = soft.tile([P, S], U8, name="e_scales", align_bytes=64)
-                nc.vector.quantize_mx(
-                    out=e_codes[h][:].bitcast(FP8X4),
-                    scales=e_scales[h][:],
-                    in_=e_grouped[:].rearrange("p j q f -> p (j q f)"),
-                )
+                    cols = slice(j0 * P, (j0 + 2) * P)
+                    nc.vector.quantize_mx(
+                        out=e_codes[h][:, cols].bitcast(FP8X4),
+                        scales=e_scales[h][:, cols],
+                        in_=e_grouped[:].rearrange("p j q f -> p (j q f)"),
+                    )
 
             def weighted_sums(h):
                 o_banks[h] = []
@@ -337,11 +340,11 @@ def tile_covenantattention_pa_kernel(
 
             def normalise_and_store(h):
                 o_sb = soft.tile([P, TILES, 2, HD], F32, bufs=4)
-                for jj in range(2):
-                    unit = h * TILES + jj
+                for j in range(2):
+                    unit = h * TILES + j
                     nc.scalar.activation(
-                        out=o_sb[:, jj, :, :].rearrange("p c d -> p (c d)"),
-                        in_=o_banks[h][0][:, jj, :],
+                        out=o_sb[:, j, :, :].rearrange("p c d -> p (c d)"),
+                        in_=o_banks[h][0][:, j, :],
                         func=FUNC.Copy,
                         scale=inv_sum[:, unit : unit + 1],
                     )

@@ -251,10 +251,10 @@ def tile_covenantattention_pa_kernel(
             psum_v = second.enter_context(tc.psum_pool(name="psum_v", bufs=2, reuse_waits="tile"))
             psum_o = second.enter_context(tc.psum_pool(name="psum_o", bufs=4, reuse_waits="tile"))
             out_views = [o.rearrange("b (p j) f -> p (b j) f", j=TILES) for o in (out_0, out_1)]
-            e_sb, e_codes, e_scales, v_codes, v_scales, o_banks = {}, {}, {}, {}, {}, {}
+            e_sb, e_codes, e_scales, v_grouped, v_codes, v_scales, o_banks = {}, {}, {}, {}, {}, {}, {}
 
             def values(h):
-                v_grouped = soft.tile([P, 2, HD, PACK], BF16, align_bytes=64)
+                v_grouped[h] = soft.tile([P, 2, HD, PACK], BF16, name="v_grouped", align_bytes=64)
                 for c_out, products in enumerate((((XR, 0), (XN, 1)), ((XR, 1), (XI, 0)))):
                     passes = [(x_sel, w_sel, g) for (x_sel, w_sel) in products for g in range(PASSES)]
                     acc = psum_v.tile([P, TILES, HD], F32)
@@ -272,17 +272,19 @@ def tile_covenantattention_pa_kernel(
                                 stop=(i == len(passes) - 1),
                             )
                     nc.vector.tensor_tensor(
-                        out=v_grouped[:, c_out, :, :],
+                        out=v_grouped[h][:, c_out, :, :],
                         in0=acc[:].rearrange("p t f -> p f t"),
                         in1=bias[c_out][:, h * HD : (h + 1) * HD].unsqueeze(2).to_broadcast([P, HD, PACK]),
                         op=ALU.add,
                     )
+
+            def quantise_values(h):
                 v_codes[h] = soft.tile([P, 2 * HD], U32, name="v_codes", align_bytes=64)
                 v_scales[h] = soft.tile([P, 2 * HD], U8, name="v_scales", align_bytes=64)
                 nc.vector.quantize_mx(
                     out=v_codes[h][:].bitcast(FP8X4),
                     scales=v_scales[h][:],
-                    in_=v_grouped[:].rearrange("p c f t -> p (c f t)"),
+                    in_=v_grouped[h][:].rearrange("p c f t -> p (c f t)"),
                 )
 
             def exponentials(h):
@@ -303,6 +305,7 @@ def tile_covenantattention_pa_kernel(
                 e_words = e_sb[h][:].bitcast(F32)
                 e_codes[h] = soft.tile([P, S], U32, name="e_codes", align_bytes=64)
                 e_scales[h] = soft.tile([P, S], U8, name="e_scales", align_bytes=64)
+                e_grouped = soft.tile([P, TILES, P, PACK], BF16, align_bytes=64)
                 for j0 in range(0, TILES, 2):
                     e_bank = psum_e.tile([P, 2, 2, P], F32)
                     for jj in range(2):
@@ -310,15 +313,16 @@ def tile_covenantattention_pa_kernel(
                             nc.tensor.transpose(
                                 e_bank[:, jj, u, :], e_words[:, j0 + jj, u * P : (u + 1) * P], ident_f32[:]
                             )
-                    e_grouped = soft.tile([P, 2, P, PACK], BF16, align_bytes=64)
                     nc.vector.tensor_copy(
-                        out=e_grouped[:].bitcast(F32), in_=e_bank[:].rearrange("p j u q -> p j q u")
+                        out=e_grouped[:, j0 : j0 + 2, :, :].bitcast(F32),
+                        in_=e_bank[:].rearrange("p j u q -> p j q u"),
                     )
+                for j0 in range(0, TILES, 2):
                     cols = slice(j0 * P, (j0 + 2) * P)
                     nc.vector.quantize_mx(
                         out=e_codes[h][:, cols].bitcast(FP8X4),
                         scales=e_scales[h][:, cols],
-                        in_=e_grouped[:].rearrange("p j q f -> p (j q f)"),
+                        in_=e_grouped[:, j0 : j0 + 2, :, :].rearrange("p j q f -> p (j q f)"),
                     )
 
             def weighted_sums(h):
@@ -360,6 +364,7 @@ def tile_covenantattention_pa_kernel(
 
             exponentials(0)
             values(0)
+            quantise_values(0)
             for h in range(H):
                 transpose_e(h)
                 if h + 1 < H:
@@ -368,4 +373,6 @@ def tile_covenantattention_pa_kernel(
                 weighted_sums(h)
                 if h >= 1:
                     normalise_and_store(h - 1)
+                if h + 1 < H:
+                    quantise_values(h + 1)
             normalise_and_store(H - 1)

@@ -27,11 +27,17 @@ PASS_COLS = PASSES * P
 XR, XI, XN = 0, 1, 2
 
 W_BUFS = 4
+QK_BUFS = 4
+V_AHEAD = 2
 SQUARE_LAG = 1
-SQRT_LAG = 3
-MAX_LAG = 4
-X_SLOT, QK_SLOT, W_SLOT = 0, 1, 3
-X_FIRST_HEAD = 3
+SQRT_LAG = 4
+MAX_LAG = 5
+QK_SLOT, SIDE_SLOT, SECOND_SIDE_SLOT = 1, 3, 0
+QK_FIRST = 2
+XQ_STEPS = (18, 22, 26)
+WQ_STEPS = (30, 31)
+V_STEPS = (32, 33)
+VQ_STEPS = (34, 35)
 
 FLOPS = 4 * 2 * S * DX * D + 4 * H * 2 * S * S * HD + 2 * H * 2 * S * S * HD
 
@@ -59,6 +65,8 @@ def tile_covenantattention_pa_kernel(
         ctx.enter_context(tc.manual_schedule())
         const = ctx.enter_context(tc.tile_pool(name="const", bufs=1))
         keep = ctx.enter_context(tc.tile_pool(name="keep", bufs=1))
+        v_pool = ctx.enter_context(tc.tile_pool(name="v_pool", bufs=V_AHEAD + 1))
+        v_grouped, v_codes, v_scales = {}, {}, {}
 
         ident_bf = const.tile([P, P], BF16)
         make_identity(nc, ident_bf[:])
@@ -77,40 +85,78 @@ def tile_covenantattention_pa_kernel(
         x_scales = keep.tile([P, 3, TILES * PASS_COLS], U8, align_bytes=64)
         w_codes = keep.tile([P, H, 2 * PASS_COLS], U32, align_bytes=64)
         w_scales = keep.tile([P, H, 2 * PASS_COLS], U8, align_bytes=64)
+        w_grouped = keep.tile([P, H, 2, PASS_COLS * PACK], BF16, align_bytes=64)
+        x_grouped_r = keep.tile([P, TILES, PASS_COLS * PACK], BF16, align_bytes=64)
+        x_grouped_i = keep.tile([P, TILES, PASS_COLS * PACK], BF16, align_bytes=64)
         bias_r = keep.tile([P, D], BF16)
         bias_i = keep.tile([P, D], BF16)
         bias = (bias_r, bias_i)
 
+        def quantise_w(h):
+            nc.vector.quantize_mx(
+                out=w_codes[:, h, :].bitcast(FP8X4),
+                scales=w_scales[:, h, :],
+                in_=w_grouped[:, h, :, :].rearrange("p c w -> p (c w)"),
+            )
+
+        def values(h, pool):
+            v_grouped[h] = v_pool.tile([P, 2, HD, PACK], BF16, name="v_grouped", align_bytes=64)
+            for c_out, products in enumerate((((XR, 0), (XN, 1)), ((XR, 1), (XI, 0)))):
+                passes = [(x_sel, w_sel, g) for (x_sel, w_sel) in products for g in range(PASSES)]
+                acc = pool.tile([P, TILES, HD], F32, tag="bank")
+                for t in range(TILES):
+                    for i, (x_sel, w_sel, g) in enumerate(passes):
+                        x_cols = slice((t * PASSES + g) * P, (t * PASSES + g + 1) * P)
+                        w_cols = slice((w_sel * PASSES + g) * P, (w_sel * PASSES + g + 1) * P)
+                        nc.tensor.matmul_mx(
+                            out=acc[:, t, :],
+                            lhsT=x_codes[:, x_sel, x_cols].bitcast(FP8X4),
+                            lhsT_scale=x_scales[:, x_sel, x_cols],
+                            rhs=w_codes[:, h, w_cols].bitcast(FP8X4),
+                            rhs_scale=w_scales[:, h, w_cols],
+                            start=(i == 0),
+                            stop=(i == len(passes) - 1),
+                        )
+                nc.vector.tensor_tensor(
+                    out=v_grouped[h][:, c_out, :, :],
+                    in0=acc[:].rearrange("p t f -> p f t"),
+                    in1=bias[c_out][:, h * HD : (h + 1) * HD].unsqueeze(2).to_broadcast([P, HD, PACK]),
+                    op=ALU.add,
+                )
+
+        def quantise_values(h):
+            v_codes[h] = v_pool.tile([P, 2 * HD], U32, name="v_codes", align_bytes=64)
+            v_scales[h] = v_pool.tile([P, 2 * HD], U8, name="v_scales", align_bytes=64)
+            nc.vector.quantize_mx(
+                out=v_codes[h][:].bitcast(FP8X4),
+                scales=v_scales[h][:],
+                in_=v_grouped[h][:].rearrange("p c f t -> p (c f t)"),
+            )
+
         with ExitStack() as first:
             raw = first.enter_context(tc.tile_pool(name="raw", bufs=1))
             w_in = first.enter_context(tc.tile_pool(name="w_in", bufs=W_BUFS))
+            qk_in = first.enter_context(tc.tile_pool(name="qk_in", bufs=QK_BUFS))
             stage = first.enter_context(tc.tile_pool(name="stage", bufs=2))
             squares = first.enter_context(tc.tile_pool(name="squares", bufs=4))
             psum_s = first.enter_context(tc.psum_pool(name="psum_s", bufs=2))
             psum_t = first.enter_context(tc.psum_pool(name="psum_t", bufs=4))
 
-            q_raw_r = raw.tile([P, H, S], BF16)
-            q_raw_i = raw.tile([P, H, S], BF16)
-            k_raw_r = raw.tile([P, UNITS, HD], BF16)
-            k_raw_i = raw.tile([P, UNITS, HD], BF16)
             x_raw_r = raw.tile([P, TILES, DX], BF16)
             x_raw_i = raw.tile([P, TILES, DX], BF16)
-            x_grouped_r = raw.tile([P, TILES, PASS_COLS * PACK], BF16, align_bytes=64)
-            x_grouped_i = raw.tile([P, TILES, PASS_COLS * PACK], BF16, align_bytes=64)
-            q_raw = (q_raw_r, q_raw_i)
-            k_raw = (k_raw_r, k_raw_i)
             x_raw = (x_raw_r, x_raw_i)
             x_grouped = (x_grouped_r, x_grouped_i)
-            w_raw, w_grouped, q_t, k_t, k_i_neg, s_r, s_i = {}, {}, {}, {}, {}, {}, {}
+            w_raw, q_raw, k_raw, q_t, k_t, k_i_neg, s_r, s_i = {}, {}, {}, {}, {}, {}, {}, {}
 
             def load_qk(h):
+                k_raw[h] = qk_in.tile([P, 2, TILES, HD], BF16, name="k_raw")
+                q_raw[h] = qk_in.tile([P, 2, S], BF16, name="q_raw")
                 for c, src in enumerate((k_zeta_r, k_zeta_i)):
                     view = src.rearrange("b h (j p) d -> p (b h j) d", p=P)
-                    units = slice(h * TILES, (h + 1) * TILES)
-                    nc.sync.dma_start(out=k_raw[c][:, units, :], in_=view[:, units, :])
+                    nc.sync.dma_start(out=k_raw[h][:, c, :, :], in_=view[:, h * TILES : (h + 1) * TILES, :])
                 for c, src in enumerate((q_zeta_r, q_zeta_i)):
                     view = src.rearrange("b h (p j) d -> p (b h) (j d)", j=TILES)
-                    nc.sync.dma_start(out=q_raw[c][:, h, :], in_=view[:, h, :])
+                    nc.sync.dma_start(out=q_raw[h][:, c, :], in_=view[:, h, :])
 
             def load_w(h):
                 w_raw[h] = w_in.tile([P, 2, DX], BF16, name="w_raw")
@@ -123,37 +169,32 @@ def tile_covenantattention_pa_kernel(
                 for c in range(2):
                     for j in range(TILES):
                         nc.tensor.transpose(
-                            k_bank[:, c, j * P : (j + 1) * P], k_raw[c][:, h * TILES + j, :], ident_bf[:]
+                            k_bank[:, c, j * P : (j + 1) * P], k_raw[h][:, c, j, :], ident_bf[:]
                         )
                 for c in range(2):
                     for j in range(TILES):
                         cols = slice(j * P, (j + 1) * P)
-                        nc.tensor.transpose(q_bank[:, c, cols], q_raw[c][:, h, cols], ident_bf[:])
+                        nc.tensor.transpose(q_bank[:, c, cols], q_raw[h][:, c, cols], ident_bf[:])
                 k_t[h] = stage.tile([P, 2, S], BF16, name="k_t")
                 k_i_neg[h] = stage.tile([P, S], BF16, name="k_i_neg")
                 q_t[h] = stage.tile([P, 2, S], BF16, name="q_t")
+                first_cols = P if h == 0 else 0
+                if first_cols:
+                    nc.scalar.copy(out=q_t[h][:, :, :first_cols], in_=q_bank[:, :, :first_cols])
                 nc.vector.tensor_copy(out=k_t[h][:], in_=k_bank[:])
                 nc.vector.tensor_scalar(
                     out=k_i_neg[h][:], in0=k_bank[:, 1, :], scalar1=-1.0, scalar2=None, op0=ALU.mult
                 )
-                nc.vector.tensor_copy(out=q_t[h][:], in_=q_bank[:])
+                nc.vector.tensor_copy(out=q_t[h][:, :, first_cols:], in_=q_bank[:, :, first_cols:])
 
             def prepare_w(h):
-                w_grouped[h] = stage.tile([P, 2, PASS_COLS * PACK], BF16, name="w_grouped", align_bytes=64)
                 banks = []
                 for c in range(2):
                     w_bank = psum_t.tile([P, PASSES, 2, P], F32, tag="bank")
                     transpose_words(nc, w_bank, w_raw[h][:, c, :], ident_f32)
                     banks.append(w_bank)
                 for c in range(2):
-                    regroup_words(nc, w_grouped[h][:, c, :], banks[c])
-
-            def quantise_w(h):
-                nc.vector.quantize_mx(
-                    out=w_codes[:, h, :].bitcast(FP8X4),
-                    scales=w_scales[:, h, :],
-                    in_=w_grouped[h][:].rearrange("p c w -> p (c w)"),
-                )
+                    regroup_words(nc, w_grouped[:, h, c, :], banks[c])
 
             def prepare_x(t):
                 banks = []
@@ -201,38 +242,35 @@ def tile_covenantattention_pa_kernel(
                 nc.vector.tensor_reduce(
                     out=max_all[:, unit : unit + 1], in_=m_all[:, unit, :], axis=AXIS.X, op=ALU.max
                 )
-                if unit % TILES == TILES - 1:
-                    head = slice(unit + 1 - TILES, unit + 1)
-                    nc.vector.tensor_scalar(
-                        out=neg_max[:, head], in0=max_all[:, head], scalar1=-1.0, scalar2=None, op0=ALU.mult
+
+            def load_x():
+                for c, src in enumerate((x_real, x_imag)):
+                    nc.sync.dma_start(
+                        out=x_raw[c][:].rearrange("p (u e) k -> p u (e k)", e=2),
+                        in_=src.rearrange("b (u p e) k -> p (b u) (e k)", p=P, e=2),
                     )
 
-            for h in range(W_BUFS):
+            for h in range(QK_FIRST):
                 load_qk(h)
+            load_x()
+            for h in range(H):
+                if h + QK_FIRST < H:
+                    load_qk(h + QK_FIRST)
                 load_w(h)
-            for c, src in enumerate((x_real, x_imag)):
-                nc.sync.dma_start(
-                    out=x_raw[c][:].rearrange("p (u e) k -> p u (e k)", e=2),
-                    in_=src.rearrange("b (u p e) k -> p (b u) (e k)", p=P, e=2),
-                )
-            for h in range(W_BUFS, H):
-                load_qk(h)
             nc.sync.dma_start(out=bias_r[:], in_=bv_r.partition_broadcast(P))
             nc.sync.dma_start(out=bias_i[:], in_=bv_i.partition_broadcast(P))
 
-            x_done = (X_FIRST_HEAD + TILES - 1) * TILES + X_SLOT
             transpose_qk(0)
+            side_jobs = [(prepare_x, t) for t in range(TILES)] + [(prepare_w, n) for n in range(H)]
             for step in range(UNITS + MAX_LAG):
                 h, j = divmod(step, TILES)
                 if step < UNITS:
-                    if j == X_SLOT and 0 <= h - X_FIRST_HEAD < TILES:
-                        prepare_x(h - X_FIRST_HEAD)
                     if j == QK_SLOT and h + 1 < H:
                         transpose_qk(h + 1)
-                    if j == W_SLOT:
-                        prepare_w(h)
-                        if h + W_BUFS < H:
-                            load_w(h + W_BUFS)
+                    if j == SIDE_SLOT or (j == SECOND_SIDE_SLOT and h >= TILES):
+                        job, which = side_jobs[0]
+                        side_jobs.remove(side_jobs[0])
+                        job(which)
                     scores(step)
                 if 0 <= step - SQUARE_LAG < UNITS:
                     squared_magnitude(step - SQUARE_LAG)
@@ -240,10 +278,14 @@ def tile_covenantattention_pa_kernel(
                     magnitude(step - SQRT_LAG)
                 if 0 <= step - MAX_LAG < UNITS:
                     maximum(step - MAX_LAG)
-                if step < UNITS and j == W_SLOT:
-                    quantise_w(h)
-                if 0 <= step - x_done < 3:
-                    quantise_x(step - x_done)
+                if step in XQ_STEPS:
+                    quantise_x((XR, XI, XN)[XQ_STEPS.index(step)])
+                if step in WQ_STEPS:
+                    quantise_w(WQ_STEPS.index(step))
+                if step in V_STEPS:
+                    values(V_STEPS.index(step), psum_t)
+                if step in VQ_STEPS:
+                    quantise_values(VQ_STEPS.index(step))
 
         with ExitStack() as second:
             soft = second.enter_context(tc.tile_pool(name="soft", bufs=2, reuse_waits="tile"))
@@ -251,44 +293,12 @@ def tile_covenantattention_pa_kernel(
             psum_v = second.enter_context(tc.psum_pool(name="psum_v", bufs=2, reuse_waits="tile"))
             psum_o = second.enter_context(tc.psum_pool(name="psum_o", bufs=4, reuse_waits="tile"))
             out_views = [o.rearrange("b (p j) f -> p (b j) f", j=TILES) for o in (out_0, out_1)]
-            e_sb, e_codes, e_scales, v_grouped, v_codes, v_scales, o_banks = {}, {}, {}, {}, {}, {}, {}
-
-            def values(h):
-                v_grouped[h] = soft.tile([P, 2, HD, PACK], BF16, name="v_grouped", align_bytes=64)
-                for c_out, products in enumerate((((XR, 0), (XN, 1)), ((XR, 1), (XI, 0)))):
-                    passes = [(x_sel, w_sel, g) for (x_sel, w_sel) in products for g in range(PASSES)]
-                    acc = psum_v.tile([P, TILES, HD], F32)
-                    for t in range(TILES):
-                        for i, (x_sel, w_sel, g) in enumerate(passes):
-                            x_cols = slice((t * PASSES + g) * P, (t * PASSES + g + 1) * P)
-                            w_cols = slice((w_sel * PASSES + g) * P, (w_sel * PASSES + g + 1) * P)
-                            nc.tensor.matmul_mx(
-                                out=acc[:, t, :],
-                                lhsT=x_codes[:, x_sel, x_cols].bitcast(FP8X4),
-                                lhsT_scale=x_scales[:, x_sel, x_cols],
-                                rhs=w_codes[:, h, w_cols].bitcast(FP8X4),
-                                rhs_scale=w_scales[:, h, w_cols],
-                                start=(i == 0),
-                                stop=(i == len(passes) - 1),
-                            )
-                    nc.vector.tensor_tensor(
-                        out=v_grouped[h][:, c_out, :, :],
-                        in0=acc[:].rearrange("p t f -> p f t"),
-                        in1=bias[c_out][:, h * HD : (h + 1) * HD].unsqueeze(2).to_broadcast([P, HD, PACK]),
-                        op=ALU.add,
-                    )
-
-            def quantise_values(h):
-                v_codes[h] = soft.tile([P, 2 * HD], U32, name="v_codes", align_bytes=64)
-                v_scales[h] = soft.tile([P, 2 * HD], U8, name="v_scales", align_bytes=64)
-                nc.vector.quantize_mx(
-                    out=v_codes[h][:].bitcast(FP8X4),
-                    scales=v_scales[h][:],
-                    in_=v_grouped[h][:].rearrange("p c f t -> p (c f t)"),
-                )
+            e_sb, e_codes, e_scales, o_banks = {}, {}, {}, {}
 
             def exponentials(h):
-                e_sb[h] = soft.tile([P, TILES, S], BF16, name="e_sb")
+                e_sb[h] = soft.tile([P, TILES, S], BF16, name="e_sb", bufs=3)
+                head = slice(h * TILES, (h + 1) * TILES)
+                nc.scalar.activation(out=neg_max[:, head], in_=max_all[:, head], func=FUNC.Copy, scale=-1.0)
                 for j in range(TILES):
                     unit = h * TILES + j
                     nc.scalar.activation(
@@ -313,10 +323,13 @@ def tile_covenantattention_pa_kernel(
                             nc.tensor.transpose(
                                 e_bank[:, jj, u, :], e_words[:, j0 + jj, u * P : (u + 1) * P], ident_f32[:]
                             )
-                    nc.vector.tensor_copy(
+                    copy = nc.scalar.copy if j0 == 0 else nc.vector.tensor_copy
+                    copy(
                         out=e_grouped[:, j0 : j0 + 2, :, :].bitcast(F32),
                         in_=e_bank[:].rearrange("p j u q -> p j q u"),
                     )
+                if h + V_AHEAD < H:
+                    quantise_w(h + V_AHEAD)
                 for j0 in range(0, TILES, 2):
                     cols = slice(j0 * P, (j0 + 2) * P)
                     nc.vector.quantize_mx(
@@ -363,16 +376,18 @@ def tile_covenantattention_pa_kernel(
                     nc.sync.dma_start(out=out_views[c][:, :, h * HD : (h + 1) * HD], in_=o_sb[:, :, c, :])
 
             exponentials(0)
-            values(0)
-            quantise_values(0)
+            transpose_e(0)
+            exponentials(1)
             for h in range(H):
-                transpose_e(h)
                 if h + 1 < H:
-                    exponentials(h + 1)
-                    values(h + 1)
+                    transpose_e(h + 1)
+                if h + 2 < H:
+                    exponentials(h + 2)
+                if h + V_AHEAD < H:
+                    values(h + V_AHEAD, psum_v)
                 weighted_sums(h)
                 if h >= 1:
                     normalise_and_store(h - 1)
-                if h + 1 < H:
-                    quantise_values(h + 1)
+                if h + V_AHEAD < H:
+                    quantise_values(h + V_AHEAD)
             normalise_and_store(H - 1)

@@ -28,6 +28,7 @@ XR, XI, XN = 0, 1, 2
 
 W_BUFS = 4
 QK_BUFS = 4
+WARM_UP = 4
 V_AHEAD = 2
 SQUARE_LAG = 1
 SQRT_LAG = 4
@@ -75,6 +76,8 @@ def tile_covenantattention_pa_kernel(
         warm = const.tile([P, 1], F32)
         nc.vector.memset(warm[:], 1.0)
         nc.scalar.activation(out=warm[:], in_=warm[:], func=FUNC.Sqrt)
+        zeros = const.tile([P, S], BF16)
+        nc.vector.memset(zeros[:], 0.0)
 
         m_all = keep.tile([P, UNITS, S], F32)
         max_all = keep.tile([P, UNITS], F32)
@@ -260,6 +263,9 @@ def tile_covenantattention_pa_kernel(
             nc.sync.dma_start(out=bias_r[:], in_=bv_r.partition_broadcast(P))
             nc.sync.dma_start(out=bias_i[:], in_=bv_i.partition_broadcast(P))
 
+            warm_bank = psum_t.tile([P, S], F32, tag="bank")
+            for n in range(WARM_UP):
+                nc.tensor.matmul(warm_bank[:], lhsT=zeros[:, :P], rhs=zeros[:], start=True, stop=True)
             transpose_qk(0)
             side_jobs = [(prepare_x, t) for t in range(TILES)] + [(prepare_w, n) for n in range(H)]
             for step in range(UNITS + MAX_LAG):

@@ -33,12 +33,13 @@ V_AHEAD = 2
 SQUARE_LAG = 1
 SQRT_LAG = 4
 MAX_LAG = 5
-QK_SLOT, SIDE_SLOT, SECOND_SIDE_SLOT = 1, 3, 0
-QK_FIRST = 2
-XQ_STEPS = (18, 22, 26)
-WQ_STEPS = (30, 31)
+QK_SLOT, QK_FIRST_SLOT = 1, 2
+SIDE_FIRST = 8
+QK_FIRST = 4
+XQ_STEPS = (15, 17, 25)
+WQ_STEPS = (21, 31)
 V_STEPS = (32, 33)
-VQ_STEPS = (34, 35)
+VQ_STEPS = (33, 34)
 
 FLOPS = 4 * 2 * S * DX * D + 4 * H * 2 * S * S * HD + 2 * H * 2 * S * S * HD
 
@@ -271,9 +272,9 @@ def tile_covenantattention_pa_kernel(
             for step in range(UNITS + MAX_LAG):
                 h, j = divmod(step, TILES)
                 if step < UNITS:
-                    if j == QK_SLOT and h + 1 < H:
+                    if j == (QK_FIRST_SLOT if h == 0 else QK_SLOT) and h + 1 < H:
                         transpose_qk(h + 1)
-                    if j == SIDE_SLOT or (j == SECOND_SIDE_SLOT and h >= TILES):
+                    if step >= SIDE_FIRST and step % 2 == 0:
                         job, which = side_jobs[0]
                         side_jobs.remove(side_jobs[0])
                         job(which)
@@ -299,7 +300,7 @@ def tile_covenantattention_pa_kernel(
             psum_v = second.enter_context(tc.psum_pool(name="psum_v", bufs=2, reuse_waits="tile"))
             psum_o = second.enter_context(tc.psum_pool(name="psum_o", bufs=4, reuse_waits="tile"))
             out_views = [o.rearrange("b (p j) f -> p (b j) f", j=TILES) for o in (out_0, out_1)]
-            e_sb, e_codes, e_scales, o_banks = {}, {}, {}, {}
+            e_sb, e_grouped, e_banks, e_codes, e_scales, o_banks = {}, {}, {}, {}, {}, {}
 
             def exponentials(h):
                 e_sb[h] = soft.tile([P, TILES, S], BF16, name="e_sb", bufs=3)
@@ -316,32 +317,35 @@ def tile_covenantattention_pa_kernel(
                     )
 
             def transpose_e(h):
-                units = slice(h * TILES, (h + 1) * TILES)
-                nc.vector.reciprocal(out=inv_sum[:, units], in_=sum_all[:, units])
                 e_words = e_sb[h][:].bitcast(F32)
-                e_codes[h] = soft.tile([P, S], U32, name="e_codes", align_bytes=64)
-                e_scales[h] = soft.tile([P, S], U8, name="e_scales", align_bytes=64)
-                e_grouped = soft.tile([P, TILES, P, PACK], BF16, align_bytes=64)
+                e_grouped[h] = soft.tile([P, TILES, P, PACK], BF16, name="e_grouped", align_bytes=64)
+                e_banks[h] = []
                 for j0 in range(0, TILES, 2):
-                    e_bank = psum_e.tile([P, 2, 2, P], F32)
+                    e_bank = psum_e.tile([P, 2, 2, P], F32, tag="bank")
                     for jj in range(2):
                         for u in range(2):
                             nc.tensor.transpose(
                                 e_bank[:, jj, u, :], e_words[:, j0 + jj, u * P : (u + 1) * P], ident_f32[:]
                             )
-                    copy = nc.scalar.copy if j0 == 0 else nc.vector.tensor_copy
-                    copy(
-                        out=e_grouped[:, j0 : j0 + 2, :, :].bitcast(F32),
-                        in_=e_bank[:].rearrange("p j u q -> p j q u"),
-                    )
-                if h + V_AHEAD < H:
-                    quantise_w(h + V_AHEAD)
-                for j0 in range(0, TILES, 2):
-                    cols = slice(j0 * P, (j0 + 2) * P)
+                    e_banks[h].append(e_bank)
+
+            def copy_e(h, half, copy):
+                j0 = 2 * half
+                copy(
+                    out=e_grouped[h][:, j0 : j0 + 2, :, :].bitcast(F32),
+                    in_=e_banks[h][half][:].rearrange("p j u q -> p j q u"),
+                )
+
+            def quantise_e(h):
+                units = slice(h * TILES, (h + 1) * TILES)
+                nc.vector.reciprocal(out=inv_sum[:, units], in_=sum_all[:, units])
+                e_codes[h] = soft.tile([P, S], U32, name="e_codes", align_bytes=64)
+                e_scales[h] = soft.tile([P, S], U8, name="e_scales", align_bytes=64)
+                for cols in (slice(0, S // 2), slice(S // 2, S)):
                     nc.vector.quantize_mx(
                         out=e_codes[h][:, cols].bitcast(FP8X4),
                         scales=e_scales[h][:, cols],
-                        in_=e_grouped[:, j0 : j0 + 2, :, :].rearrange("p j q f -> p (j q f)"),
+                        in_=e_grouped[h][:].rearrange("p j q f -> p (j q f)")[:, PACK * cols.start : PACK * cols.stop],
                     )
 
             def weighted_sums(h):
@@ -381,14 +385,21 @@ def tile_covenantattention_pa_kernel(
                 for c in range(2):
                     nc.sync.dma_start(out=out_views[c][:, :, h * HD : (h + 1) * HD], in_=o_sb[:, :, c, :])
 
+            def prepare_e(h):
+                transpose_e(h)
+                copy_e(h, 1, nc.vector.tensor_copy)
+                copy_e(h, 0, nc.scalar.copy)
+                if h + 1 < H:
+                    exponentials(h + 1)
+                if h + V_AHEAD < H:
+                    quantise_w(h + V_AHEAD)
+                quantise_e(h)
+
             exponentials(0)
-            transpose_e(0)
-            exponentials(1)
+            prepare_e(0)
             for h in range(H):
                 if h + 1 < H:
-                    transpose_e(h + 1)
-                if h + 2 < H:
-                    exponentials(h + 2)
+                    prepare_e(h + 1)
                 if h + V_AHEAD < H:
                     values(h + V_AHEAD, psum_v)
                 weighted_sums(h)

@@ -28,6 +28,7 @@ XR, XI, XN = 0, 1, 2
 
 W_BUFS = 4
 QK_BUFS = 4
+EXP_LEAD = 2
 WARM_UP = 4
 V_AHEAD = 2
 SQUARE_LAG = 1
@@ -37,7 +38,7 @@ QK_SLOT, QK_FIRST_SLOT = 1, 2
 SIDE_FIRST = 8
 QK_FIRST = 4
 XQ_STEPS = (15, 17, 25)
-WQ_STEPS = (21, 31)
+WQ_STEPS = (21, 28)
 V_STEPS = (32, 33)
 VQ_STEPS = (33, 34)
 
@@ -155,12 +156,11 @@ def tile_covenantattention_pa_kernel(
             def load_qk(h):
                 k_raw[h] = qk_in.tile([P, 2, TILES, HD], BF16, name="k_raw")
                 q_raw[h] = qk_in.tile([P, 2, S], BF16, name="q_raw")
-                for c, src in enumerate((k_zeta_r, k_zeta_i)):
-                    view = src.rearrange("b h (j p) d -> p (b h j) d", p=P)
-                    nc.sync.dma_start(out=k_raw[h][:, c, :, :], in_=view[:, h * TILES : (h + 1) * TILES, :])
-                for c, src in enumerate((q_zeta_r, q_zeta_i)):
-                    view = src.rearrange("b h (p j) d -> p (b h) (j d)", j=TILES)
-                    nc.sync.dma_start(out=q_raw[h][:, c, :], in_=view[:, h, :])
+                for c, (k_src, q_src) in enumerate(((k_zeta_r, q_zeta_r), (k_zeta_i, q_zeta_i))):
+                    k_view = k_src.rearrange("b h (j p) d -> p (b h j) d", p=P)
+                    q_view = q_src.rearrange("b h (p j) d -> p (b h) (j d)", j=TILES)
+                    nc.sync.dma_start(out=k_raw[h][:, c, :, :], in_=k_view[:, h * TILES : (h + 1) * TILES, :])
+                    nc.sync.dma_start(out=q_raw[h][:, c, :], in_=q_view[:, h, :])
 
             def load_w(h):
                 w_raw[h] = w_in.tile([P, 2, DX], BF16, name="w_raw")
@@ -182,14 +182,30 @@ def tile_covenantattention_pa_kernel(
                 k_t[h] = stage.tile([P, 2, S], BF16, name="k_t")
                 k_i_neg[h] = stage.tile([P, S], BF16, name="k_i_neg")
                 q_t[h] = stage.tile([P, 2, S], BF16, name="q_t")
-                first_cols = P if h == 0 else 0
-                if first_cols:
-                    nc.scalar.copy(out=q_t[h][:, :, :first_cols], in_=q_bank[:, :, :first_cols])
                 nc.vector.tensor_copy(out=k_t[h][:], in_=k_bank[:])
                 nc.vector.tensor_scalar(
                     out=k_i_neg[h][:], in0=k_bank[:, 1, :], scalar1=-1.0, scalar2=None, op0=ALU.mult
                 )
-                nc.vector.tensor_copy(out=q_t[h][:, :, first_cols:], in_=q_bank[:, :, first_cols:])
+                nc.vector.tensor_copy(out=q_t[h][:], in_=q_bank[:])
+
+            def transpose_first_head():
+                k_t[0] = stage.tile([P, 2, S], BF16, name="k_t")
+                k_i_neg[0] = stage.tile([P, S], BF16, name="k_i_neg")
+                q_t[0] = stage.tile([P, 2, S], BF16, name="q_t")
+                for c in range(2):
+                    k_bank = psum_t.tile([P, S], BF16, tag="bank")
+                    q_bank = psum_t.tile([P, S], BF16, tag="bank")
+                    for j in range(TILES):
+                        nc.tensor.transpose(k_bank[:, j * P : (j + 1) * P], k_raw[0][:, c, j, :], ident_bf[:])
+                    for j in range(TILES):
+                        cols = slice(j * P, (j + 1) * P)
+                        nc.tensor.transpose(q_bank[:, cols], q_raw[0][:, c, cols], ident_bf[:])
+                    nc.vector.tensor_copy(out=k_t[0][:, c, :], in_=k_bank[:])
+                    if c == 1:
+                        nc.vector.tensor_scalar(
+                            out=k_i_neg[0][:], in0=k_bank[:], scalar1=-1.0, scalar2=None, op0=ALU.mult
+                        )
+                    nc.scalar.copy(out=q_t[0][:, c, :], in_=q_bank[:])
 
             def prepare_w(h):
                 banks = []
@@ -267,7 +283,7 @@ def tile_covenantattention_pa_kernel(
             warm_bank = psum_t.tile([P, S], F32, tag="bank")
             for n in range(WARM_UP):
                 nc.tensor.matmul(warm_bank[:], lhsT=zeros[:, :P], rhs=zeros[:], start=True, stop=True)
-            transpose_qk(0)
+            transpose_first_head()
             side_jobs = [(prepare_x, t) for t in range(TILES)] + [(prepare_w, n) for n in range(H)]
             for step in range(UNITS + MAX_LAG):
                 h, j = divmod(step, TILES)
@@ -303,7 +319,7 @@ def tile_covenantattention_pa_kernel(
             e_sb, e_grouped, e_banks, e_codes, e_scales, o_banks = {}, {}, {}, {}, {}, {}
 
             def exponentials(h):
-                e_sb[h] = soft.tile([P, TILES, S], BF16, name="e_sb", bufs=3)
+                e_sb[h] = soft.tile([P, TILES, S], BF16, name="e_sb", bufs=EXP_LEAD + 2)
                 head = slice(h * TILES, (h + 1) * TILES)
                 nc.scalar.activation(out=neg_max[:, head], in_=max_all[:, head], func=FUNC.Copy, scale=-1.0)
                 for j in range(TILES):
@@ -329,9 +345,9 @@ def tile_covenantattention_pa_kernel(
                             )
                     e_banks[h].append(e_bank)
 
-            def copy_e(h, half, copy):
+            def copy_e(h, half):
                 j0 = 2 * half
-                copy(
+                nc.vector.tensor_copy(
                     out=e_grouped[h][:, j0 : j0 + 2, :, :].bitcast(F32),
                     in_=e_banks[h][half][:].rearrange("p j u q -> p j q u"),
                 )
@@ -367,35 +383,37 @@ def tile_covenantattention_pa_kernel(
 
             def normalise_and_store(h):
                 o_sb = soft.tile([P, TILES, 2, HD], F32, bufs=4)
-                for j in range(2):
+                for j in range(TILES if h < H - 1 else 2):
                     unit = h * TILES + j
                     nc.scalar.activation(
                         out=o_sb[:, j, :, :].rearrange("p c d -> p (c d)"),
-                        in_=o_banks[h][0][:, j, :],
+                        in_=o_banks[h][j // 2][:, j % 2, :],
                         func=FUNC.Copy,
                         scale=inv_sum[:, unit : unit + 1],
                     )
-                unit = h * TILES + 2
-                nc.vector.tensor_tensor(
-                    out=o_sb[:, 2:TILES, :, :].rearrange("p j c d -> p j (c d)"),
-                    in0=o_banks[h][1][:],
-                    in1=inv_sum[:, unit : unit + 2].unsqueeze(2).to_broadcast([P, 2, 2 * HD]),
-                    op=ALU.mult,
-                )
+                if h == H - 1:
+                    unit = h * TILES + 2
+                    nc.vector.tensor_tensor(
+                        out=o_sb[:, 2:TILES, :, :].rearrange("p j c d -> p j (c d)"),
+                        in0=o_banks[h][1][:],
+                        in1=inv_sum[:, unit : unit + 2].unsqueeze(2).to_broadcast([P, 2, 2 * HD]),
+                        op=ALU.mult,
+                    )
                 for c in range(2):
                     nc.sync.dma_start(out=out_views[c][:, :, h * HD : (h + 1) * HD], in_=o_sb[:, :, c, :])
 
             def prepare_e(h):
                 transpose_e(h)
-                copy_e(h, 1, nc.vector.tensor_copy)
-                copy_e(h, 0, nc.scalar.copy)
-                if h + 1 < H:
-                    exponentials(h + 1)
+                for half in range(2):
+                    copy_e(h, half)
+                if h + EXP_LEAD < H:
+                    exponentials(h + EXP_LEAD)
                 if h + V_AHEAD < H:
                     quantise_w(h + V_AHEAD)
                 quantise_e(h)
 
-            exponentials(0)
+            for h in range(EXP_LEAD):
+                exponentials(h)
             prepare_e(0)
             for h in range(H):
                 if h + 1 < H:

@@ -29,6 +29,7 @@ XR, XI, XN = 0, 1, 2
 W_BUFS = 4
 QK_BUFS = 4
 EXP_LEAD = 2
+WARM_HEADS = 2
 WARM_UP = 4
 V_AHEAD = 2
 SQUARE_LAG = 1
@@ -316,6 +317,7 @@ def tile_covenantattention_pa_kernel(
             psum_v = second.enter_context(tc.psum_pool(name="psum_v", bufs=2, reuse_waits="tile"))
             psum_o = second.enter_context(tc.psum_pool(name="psum_o", bufs=4, reuse_waits="tile"))
             out_views = [o.rearrange("b (p j) f -> p (b j) f", j=TILES) for o in (out_0, out_1)]
+            warm_bank = psum_v.tile([P, S], F32, tag="bank")
             e_sb, e_grouped, e_banks, e_codes, e_scales, o_banks = {}, {}, {}, {}, {}, {}
 
             def exponentials(h):
@@ -339,6 +341,8 @@ def tile_covenantattention_pa_kernel(
                 for j0 in range(0, TILES, 2):
                     e_bank = psum_e.tile([P, 2, 2, P], F32, tag="bank")
                     for jj in range(2):
+                        if h < WARM_HEADS:
+                            nc.tensor.matmul(warm_bank[:], lhsT=zeros[:, :P], rhs=zeros[:], start=True, stop=True)
                         for u in range(2):
                             nc.tensor.transpose(
                                 e_bank[:, jj, u, :], e_words[:, j0 + jj, u * P : (u + 1) * P], ident_f32[:]

from contextlib import ExitStack

import concourse.mybir as mybir
from concourse.masks import make_identity

F32 = mybir.dt.float32
BF16 = mybir.dt.bfloat16
U32 = mybir.dt.uint32
U8 = mybir.dt.uint8
FP8X4 = mybir.dt.float8_e4m3fn_x4
FUNC = mybir.ActivationFunctionType
ALU = mybir.AluOpType
AXIS = mybir.AxisListType

P = 128
S = 512
H = 8
HD = 128
DX = 1024
D = H * HD
PACK = 4
TILES = S // P
UNITS = H * TILES
PASSES = DX // (P * PACK)
PASS_COLS = PASSES * P

XR, XI, XN = 0, 1, 2

W_BUFS = 4
QK_BUFS = 4
EXP_LEAD = 2
WARM_HEADS = 2
WARM_UP = 4
V_AHEAD = 2
SQUARE_LAG = 1
SQRT_LAG = 4
MAX_LAG = 5
QK_SLOT, QK_FIRST_SLOT = 1, 2
SIDE_FIRST = 8
QK_FIRST = 4
XQ_STEPS = (15, 17, 25)
WQ_STEPS = (21, 28)
V_STEPS = (32, 33)
VQ_STEPS = (33, 34)

FLOPS = 4 * 2 * S * DX * D + 4 * H * 2 * S * S * HD + 2 * H * 2 * S * S * HD


def transpose_words(nc, bank, rows, ident_f32):
    words = rows.bitcast(F32)
    for g in range(PASSES):
        for u in range(2):
            first = (2 * g + u) * P
            nc.tensor.transpose(bank[:, g, u, :], words[:, first : first + P], ident_f32[:])


def regroup_words(nc, grouped, bank):
    nc.vector.tensor_copy(
        out=grouped.bitcast(F32).rearrange("p (g r u) -> p g r u", g=PASSES, u=2),
        in_=bank[:].rearrange("p g u r -> p g r u"),
    )


def tile_covenantattention_pa_kernel(
    tc, x_real, x_imag, q_zeta_r, q_zeta_i, k_zeta_r, k_zeta_i, wv_r, wv_i, bv_r, bv_i, out_0, out_1
):
    nc = tc.nc
    with ExitStack() as ctx:
        ctx.enter_context(tc.manual_schedule())
        const = ctx.enter_context(tc.tile_pool(name="const", bufs=1))
        keep = ctx.enter_context(tc.tile_pool(name="keep", bufs=1))
        v_pool = ctx.enter_context(tc.tile_pool(name="v_pool", bufs=V_AHEAD + 1))
        v_grouped, v_codes, v_scales = {}, {}, {}

        ident_bf = const.tile([P, P], BF16)
        make_identity(nc, ident_bf[:])
        ident_f32 = const.tile([P, P], F32)
        make_identity(nc, ident_f32[:])
        warm = const.tile([P, 1], F32)
        nc.vector.memset(warm[:], 1.0)
        nc.scalar.activation(out=warm[:], in_=warm[:], func=FUNC.Sqrt)
        zeros = const.tile([P, S], BF16)
        nc.vector.memset(zeros[:], 0.0)

        m_all = keep.tile([P, UNITS, S], F32)
        max_all = keep.tile([P, UNITS], F32)
        neg_max = keep.tile([P, UNITS], F32)
        sum_all = keep.tile([P, UNITS], F32)
        inv_sum = keep.tile([P, UNITS], F32)
        x_codes = keep.tile([P, 3, TILES * PASS_COLS], U32, align_bytes=64)
        x_scales = keep.tile([P, 3, TILES * PASS_COLS], U8, align_bytes=64)
        w_codes = keep.tile([P, H, 2 * PASS_COLS], U32, align_bytes=64)
        w_scales = keep.tile([P, H, 2 * PASS_COLS], U8, align_bytes=64)
        w_grouped = keep.tile([P, H, 2, PASS_COLS * PACK], BF16, align_bytes=64)
        x_grouped_r = keep.tile([P, TILES, PASS_COLS * PACK], BF16, align_bytes=64)
        x_grouped_i = keep.tile([P, TILES, PASS_COLS * PACK], BF16, align_bytes=64)
        bias_r = keep.tile([P, D], BF16)
        bias_i = keep.tile([P, D], BF16)
        bias = (bias_r, bias_i)

        def quantise_w(h):
            nc.vector.quantize_mx(
                out=w_codes[:, h, :].bitcast(FP8X4),
                scales=w_scales[:, h, :],
                in_=w_grouped[:, h, :, :].rearrange("p c w -> p (c w)"),
            )

        def values(h, pool):
            v_grouped[h] = v_pool.tile([P, 2, HD, PACK], BF16, name="v_grouped", align_bytes=64)
            for c_out, products in enumerate((((XR, 0), (XN, 1)), ((XR, 1), (XI, 0)))):
                passes = [(x_sel, w_sel, g) for (x_sel, w_sel) in products for g in range(PASSES)]
                acc = pool.tile([P, TILES, HD], F32, tag="bank")
                for t in range(TILES):
                    for i, (x_sel, w_sel, g) in enumerate(passes):
                        x_cols = slice((t * PASSES + g) * P, (t * PASSES + g + 1) * P)
                        w_cols = slice((w_sel * PASSES + g) * P, (w_sel * PASSES + g + 1) * P)
                        nc.tensor.matmul_mx(
                            out=acc[:, t, :],
                            lhsT=x_codes[:, x_sel, x_cols].bitcast(FP8X4),
                            lhsT_scale=x_scales[:, x_sel, x_cols],
                            rhs=w_codes[:, h, w_cols].bitcast(FP8X4),
                            rhs_scale=w_scales[:, h, w_cols],
                            start=(i == 0),
                            stop=(i == len(passes) - 1),
                        )
                nc.vector.tensor_tensor(
                    out=v_grouped[h][:, c_out, :, :],
                    in0=acc[:].rearrange("p t f -> p f t"),
                    in1=bias[c_out][:, h * HD : (h + 1) * HD].unsqueeze(2).to_broadcast([P, HD, PACK]),
                    op=ALU.add,
                )

        def quantise_values(h):
            v_codes[h] = v_pool.tile([P, 2 * HD], U32, name="v_codes", align_bytes=64)
            v_scales[h] = v_pool.tile([P, 2 * HD], U8, name="v_scales", align_bytes=64)
            nc.vector.quantize_mx(
                out=v_codes[h][:].bitcast(FP8X4),
                scales=v_scales[h][:],
                in_=v_grouped[h][:].rearrange("p c f t -> p (c f t)"),
            )

        with ExitStack() as first:
            raw = first.enter_context(tc.tile_pool(name="raw", bufs=1))
            w_in = first.enter_context(tc.tile_pool(name="w_in", bufs=W_BUFS))
            qk_in = first.enter_context(tc.tile_pool(name="qk_in", bufs=QK_BUFS))
            stage = first.enter_context(tc.tile_pool(name="stage", bufs=2))
            squares = first.enter_context(tc.tile_pool(name="squares", bufs=4))
            psum_s = first.enter_context(tc.psum_pool(name="psum_s", bufs=2))
            psum_t = first.enter_context(tc.psum_pool(name="psum_t", bufs=4))

            x_raw_r = raw.tile([P, TILES, DX], BF16)
            x_raw_i = raw.tile([P, TILES, DX], BF16)
            x_raw = (x_raw_r, x_raw_i)
            x_grouped = (x_grouped_r, x_grouped_i)
            w_raw, q_raw, k_raw, q_t, k_t, k_i_neg, s_r, s_i = {}, {}, {}, {}, {}, {}, {}, {}

            def load_qk(h):
                k_raw[h] = qk_in.tile([P, 2, TILES, HD], BF16, name="k_raw")
                q_raw[h] = qk_in.tile([P, 2, S], BF16, name="q_raw")
                for c, (k_src, q_src) in enumerate(((k_zeta_r, q_zeta_r), (k_zeta_i, q_zeta_i))):
                    k_view = k_src.rearrange("b h (j p) d -> p (b h j) d", p=P)
                    q_view = q_src.rearrange("b h (p j) d -> p (b h) (j d)", j=TILES)
                    nc.sync.dma_start(out=k_raw[h][:, c, :, :], in_=k_view[:, h * TILES : (h + 1) * TILES, :])
                    nc.sync.dma_start(out=q_raw[h][:, c, :], in_=q_view[:, h, :])

            def load_w(h):
                w_raw[h] = w_in.tile([P, 2, DX], BF16, name="w_raw")
                for c, src in enumerate((wv_r, wv_i)):
                    nc.sync.dma_start(out=w_raw[h][:, c, :], in_=src[h * HD : (h + 1) * HD, :])

            def transpose_qk(h):
                k_bank = psum_t.tile([P, 2, S], BF16, tag="bank")
                q_bank = psum_t.tile([P, 2, S], BF16, tag="bank")
                for c in range(2):
                    for j in range(TILES):
                        nc.tensor.transpose(
                            k_bank[:, c, j * P : (j + 1) * P], k_raw[h][:, c, j, :], ident_bf[:]
                        )
                for c in range(2):
                    for j in range(TILES):
                        cols = slice(j * P, (j + 1) * P)
                        nc.tensor.transpose(q_bank[:, c, cols], q_raw[h][:, c, cols], ident_bf[:])
                k_t[h] = stage.tile([P, 2, S], BF16, name="k_t")
                k_i_neg[h] = stage.tile([P, S], BF16, name="k_i_neg")
                q_t[h] = stage.tile([P, 2, S], BF16, name="q_t")
                nc.vector.tensor_copy(out=k_t[h][:], in_=k_bank[:])
                nc.vector.tensor_scalar(
                    out=k_i_neg[h][:], in0=k_bank[:, 1, :], scalar1=-1.0, scalar2=None, op0=ALU.mult
                )
                nc.vector.tensor_copy(out=q_t[h][:], in_=q_bank[:])

            def transpose_first_head():
                k_t[0] = stage.tile([P, 2, S], BF16, name="k_t")
                k_i_neg[0] = stage.tile([P, S], BF16, name="k_i_neg")
                q_t[0] = stage.tile([P, 2, S], BF16, name="q_t")
                for c in range(2):
                    k_bank = psum_t.tile([P, S], BF16, tag="bank")
                    q_bank = psum_t.tile([P, S], BF16, tag="bank")
                    for j in range(TILES):
                        nc.tensor.transpose(k_bank[:, j * P : (j + 1) * P], k_raw[0][:, c, j, :], ident_bf[:])
                    for j in range(TILES):
                        cols = slice(j * P, (j + 1) * P)
                        nc.tensor.transpose(q_bank[:, cols], q_raw[0][:, c, cols], ident_bf[:])
                    nc.vector.tensor_copy(out=k_t[0][:, c, :], in_=k_bank[:])
                    if c == 1:
                        nc.vector.tensor_scalar(
                            out=k_i_neg[0][:], in0=k_bank[:], scalar1=-1.0, scalar2=None, op0=ALU.mult
                        )
                    nc.scalar.copy(out=q_t[0][:, c, :], in_=q_bank[:])

            def prepare_w(h):
                banks = []
                for c in range(2):
                    w_bank = psum_t.tile([P, PASSES, 2, P], F32, tag="bank")
                    transpose_words(nc, w_bank, w_raw[h][:, c, :], ident_f32)
                    banks.append(w_bank)
                for c in range(2):
                    regroup_words(nc, w_grouped[:, h, c, :], banks[c])

            def prepare_x(t):
                banks = []
                for c in range(2):
                    x_bank = psum_t.tile([P, PASSES, 2, P], F32, tag="bank")
                    transpose_words(nc, x_bank, x_raw[c][:, t, :], ident_f32)
                    banks.append(x_bank)
                for c in range(2):
                    regroup_words(nc, x_grouped[c][:, t, :], banks[c])

            def quantise_x(x_sel):
                flat_r = x_grouped_r[:].rearrange("p t w -> p (t w)")
                flat_i = x_grouped_i[:].rearrange("p t w -> p (t w)")
                if x_sel == XN:
                    nc.vector.tensor_scalar(out=flat_r, in0=flat_i, scalar1=-1.0, scalar2=None, op0=ALU.mult)
                nc.vector.quantize_mx(
                    out=x_codes[:, x_sel, :].bitcast(FP8X4),
                    scales=x_scales[:, x_sel, :],
                    in_=flat_i if x_sel == XI else flat_r,
                )

            def scores(unit):
                h, j = divmod(unit, TILES)
                q_r = q_t[h][:, 0, j * P : (j + 1) * P]
                q_i = q_t[h][:, 1, j * P : (j + 1) * P]
                s_r[unit] = psum_s.tile([P, S], F32, name="s_r")
                s_i[unit] = psum_s.tile([P, S], F32, name="s_i")
                nc.tensor.matmul(s_r[unit][:], lhsT=q_r, rhs=k_t[h][:, 0, :], start=True, stop=False)
                nc.tensor.matmul(s_i[unit][:], lhsT=q_r, rhs=k_t[h][:, 1, :], start=True, stop=False)
                nc.tensor.matmul(s_r[unit][:], lhsT=q_i, rhs=k_i_neg[h][:], start=False, stop=True)
                nc.tensor.matmul(s_i[unit][:], lhsT=q_i, rhs=k_t[h][:, 0, :], start=False, stop=True)

            def squared_magnitude(unit):
                sq_r = squares.tile([P, S], F32)
                sq_i = squares.tile([P, S], F32)
                nc.scalar.activation(out=sq_r[:], in_=s_r[unit][:], func=FUNC.Square)
                nc.scalar.activation(out=sq_i[:], in_=s_i[unit][:], func=FUNC.Square)
                nc.gpsimd.tensor_tensor(out=m_all[:, unit, :], in0=sq_r[:], in1=sq_i[:], op=ALU.add)

            def magnitude(unit):
                m = m_all[:, unit, :]
                nc.scalar.activation(out=m, in_=m, func=FUNC.Sqrt, scale=1.0 / HD)

            def maximum(unit):
                nc.vector.tensor_reduce(
                    out=max_all[:, unit : unit + 1], in_=m_all[:, unit, :], axis=AXIS.X, op=ALU.max
                )

            def load_x():
                for c, src in enumerate((x_real, x_imag)):
                    nc.sync.dma_start(
                        out=x_raw[c][:].rearrange("p (u e) k -> p u (e k)", e=2),
                        in_=src.rearrange("b (u p e) k -> p (b u) (e k)", p=P, e=2),
                    )

            for h in range(QK_FIRST):
                load_qk(h)
            load_x()
            for h in range(H):
                if h + QK_FIRST < H:
                    load_qk(h + QK_FIRST)
                load_w(h)
            nc.sync.dma_start(out=bias_r[:], in_=bv_r.partition_broadcast(P))
            nc.sync.dma_start(out=bias_i[:], in_=bv_i.partition_broadcast(P))

            warm_bank = psum_t.tile([P, S], F32, tag="bank")
            for n in range(WARM_UP):
                nc.tensor.matmul(warm_bank[:], lhsT=zeros[:, :P], rhs=zeros[:], start=True, stop=True)
            transpose_first_head()
            side_jobs = [(prepare_x, t) for t in range(TILES)] + [(prepare_w, n) for n in range(H)]
            for step in range(UNITS + MAX_LAG):
                h, j = divmod(step, TILES)
                if step < UNITS:
                    if j == (QK_FIRST_SLOT if h == 0 else QK_SLOT) and h + 1 < H:
                        transpose_qk(h + 1)
                    if step >= SIDE_FIRST and step % 2 == 0:
                        job, which = side_jobs[0]
                        side_jobs.remove(side_jobs[0])
                        job(which)
                    scores(step)
                if 0 <= step - SQUARE_LAG < UNITS:
                    squared_magnitude(step - SQUARE_LAG)
                if 0 <= step - SQRT_LAG < UNITS:
                    magnitude(step - SQRT_LAG)
                if 0 <= step - MAX_LAG < UNITS:
                    maximum(step - MAX_LAG)
                if step in XQ_STEPS:
                    quantise_x((XR, XI, XN)[XQ_STEPS.index(step)])
                if step in WQ_STEPS:
                    quantise_w(WQ_STEPS.index(step))
                if step in V_STEPS:
                    values(V_STEPS.index(step), psum_t)
                if step in VQ_STEPS:
                    quantise_values(VQ_STEPS.index(step))

        with ExitStack() as second:
            soft = second.enter_context(tc.tile_pool(name="soft", bufs=2, reuse_waits="tile"))
            psum_e = second.enter_context(tc.psum_pool(name="psum_e", bufs=2, reuse_waits="tile"))
            psum_v = second.enter_context(tc.psum_pool(name="psum_v", bufs=2, reuse_waits="tile"))
            psum_o = second.enter_context(tc.psum_pool(name="psum_o", bufs=4, reuse_waits="tile"))
            out_views = [o.rearrange("b (p j) f -> p (b j) f", j=TILES) for o in (out_0, out_1)]
            warm_bank = psum_v.tile([P, S], F32, tag="bank")
            e_sb, e_grouped, e_banks, e_codes, e_scales, o_banks = {}, {}, {}, {}, {}, {}

            def exponentials(h):
                e_sb[h] = soft.tile([P, TILES, S], BF16, name="e_sb", bufs=EXP_LEAD + 2)
                head = slice(h * TILES, (h + 1) * TILES)
                nc.scalar.activation(out=neg_max[:, head], in_=max_all[:, head], func=FUNC.Copy, scale=-1.0)
                for j in range(TILES):
                    unit = h * TILES + j
                    nc.scalar.activation(
                        out=e_sb[h][:, j, :],
                        in_=m_all[:, unit, :],
                        func=FUNC.Exp,
                        bias=neg_max[:, unit : unit + 1],
                        accum_out=sum_all[:, unit : unit + 1],
                    )

            def transpose_e(h):
                e_words = e_sb[h][:].bitcast(F32)
                e_grouped[h] = soft.tile([P, TILES, P, PACK], BF16, name="e_grouped", align_bytes=64)
                e_banks[h] = []
                for j0 in range(0, TILES, 2):
                    e_bank = psum_e.tile([P, 2, 2, P], F32, tag="bank")
                    for jj in range(2):
                        if h < WARM_HEADS:
                            nc.tensor.matmul(warm_bank[:], lhsT=zeros[:, :P], rhs=zeros[:], start=True, stop=True)
                        for u in range(2):
                            nc.tensor.transpose(
                                e_bank[:, jj, u, :], e_words[:, j0 + jj, u * P : (u + 1) * P], ident_f32[:]
                            )
                    e_banks[h].append(e_bank)

            def copy_e(h, half):
                j0 = 2 * half
                nc.vector.tensor_copy(
                    out=e_grouped[h][:, j0 : j0 + 2, :, :].bitcast(F32),
                    in_=e_banks[h][half][:].rearrange("p j u q -> p j q u"),
                )

            def quantise_e(h):
                units = slice(h * TILES, (h + 1) * TILES)
                nc.vector.reciprocal(out=inv_sum[:, units], in_=sum_all[:, units])
                e_codes[h] = soft.tile([P, S], U32, name="e_codes", align_bytes=64)
                e_scales[h] = soft.tile([P, S], U8, name="e_scales", align_bytes=64)
                for cols in (slice(0, S // 2), slice(S // 2, S)):
                    nc.vector.quantize_mx(
                        out=e_codes[h][:, cols].bitcast(FP8X4),
                        scales=e_scales[h][:, cols],
                        in_=e_grouped[h][:].rearrange("p j q f -> p (j q f)")[:, PACK * cols.start : PACK * cols.stop],
                    )

            def weighted_sums(h):
                o_banks[h] = []
                for j0 in range(0, TILES, 2):
                    o_bank = psum_o.tile([P, 2, 2 * HD], F32)
                    for jj in range(2):
                        cols = slice((j0 + jj) * P, (j0 + jj + 1) * P)
                        nc.tensor.matmul_mx(
                            out=o_bank[:, jj, :],
                            lhsT=e_codes[h][:, cols].bitcast(FP8X4),
                            lhsT_scale=e_scales[h][:, cols],
                            rhs=v_codes[h][:].bitcast(FP8X4),
                            rhs_scale=v_scales[h][:],
                            start=True,
                            stop=True,
                        )
                    o_banks[h].append(o_bank)

            def normalise_and_store(h):
                o_sb = soft.tile([P, TILES, 2, HD], F32, bufs=4)
                for j in range(TILES if h < H - 1 else 2):
                    unit = h * TILES + j
                    nc.scalar.activation(
                        out=o_sb[:, j, :, :].rearrange("p c d -> p (c d)"),
                        in_=o_banks[h][j // 2][:, j % 2, :],
                        func=FUNC.Copy,
                        scale=inv_sum[:, unit : unit + 1],
                    )
                if h == H - 1:
                    unit = h * TILES + 2
                    nc.vector.tensor_tensor(
                        out=o_sb[:, 2:TILES, :, :].rearrange("p j c d -> p j (c d)"),
                        in0=o_banks[h][1][:],
                        in1=inv_sum[:, unit : unit + 2].unsqueeze(2).to_broadcast([P, 2, 2 * HD]),
                        op=ALU.mult,
                    )
                for c in range(2):
                    nc.sync.dma_start(out=out_views[c][:, :, h * HD : (h + 1) * HD], in_=o_sb[:, :, c, :])

            def prepare_e(h):
                transpose_e(h)
                for half in range(2):
                    copy_e(h, half)
                if h + EXP_LEAD < H:
                    exponentials(h + EXP_LEAD)
                if h + V_AHEAD < H:
                    quantise_w(h + V_AHEAD)
                quantise_e(h)

            for h in range(EXP_LEAD):
                exponentials(h)
            prepare_e(0)
            for h in range(H):
                if h + 1 < H:
                    prepare_e(h + 1)
                if h + V_AHEAD < H:
                    values(h + V_AHEAD, psum_v)
                weighted_sums(h)
                if h >= 1:
                    normalise_and_store(h - 1)
                if h + V_AHEAD < H:
                    quantise_values(h + V_AHEAD)
            normalise_and_store(H - 1)
